import numpy as np
import ml_dtypes


def mxq(x, axis, fmt="e4m3"):
    dtype, down = {"e4m3": (ml_dtypes.float8_e4m3fn, 7), "e5m2": (ml_dtypes.float8_e5m2, 14)}[fmt]
    v = np.moveaxis(np.asarray(x, np.float32).astype(ml_dtypes.bfloat16).astype(np.float64), axis, -1)
    blocks = v.reshape(v.shape[:-1] + (-1, 32))
    amax = np.abs(blocks).max(-1, keepdims=True)
    byte = np.maximum(np.where(amax > 0, np.frexp(amax)[1] - 1 + 127, 0) - down, 1)
    scale = np.exp2(byte - 127.0)
    codes = (blocks / scale).astype(np.float32).astype(dtype).astype(np.float64)
    return np.moveaxis((codes * scale).reshape(v.shape), -1, axis)


WIDE = False


def mx_kscale(k):
    if not WIDE:
        return np.ones(k)
    levels = np.array([10, -10, 5, -5, 0])
    a = np.random.permutation(np.resize(levels, k // 512 * 4)).reshape(k // 512, 4)
    idx = np.arange(k)
    return np.exp2(a[idx // 512, idx % 128 // 32])


BF16 = ml_dtypes.bfloat16


def bf(x):
    return np.asarray(x, np.float32).astype(BF16)


def f64(x):
    return np.asarray(x).astype(np.float64)


B, IN, NLVL, KLVL, C, CM, CO, OU, OV = 2, 256, 5, 2, 128, 128, 128, 8, 8
NK = 2 ** KLVL
S = 2 ** (NLVL - KLVL)
KA, KB = 4 * C, 4 * CM


def patches(x):
    U, V, Bn, H, W, Cc = x.shape
    return x.reshape(U, V, Bn, H // 2, 2, W // 2, 2, Cc).swapaxes(4, 5).reshape(U, V, Bn * (H // 2) * (W // 2), 4 * Cc)


def node_conv(x, w, b):
    U, V, Bn, H, W, Cc = x.shape
    Co = w.shape[-1]
    y = (mxq(patches(x), 3, "e4m3") @ mxq(w.reshape(U, V, 4 * Cc, Co), 2, "e4m3")) + b[:, :, None, :]
    return np.maximum(y, 0.0).reshape(U, V, Bn, H // 2, W // 2, Co)


def setup_inputs():
    s = mx_kscale(KA).reshape(2, 2, C)
    t = mx_kscale(KB)[:CM]
    x = np.maximum(np.random.standard_normal((NK, NK, B, S, S, C)), 0.0) * np.tile(s, (S // 2, S // 2, 1))
    return {"x_leaf": bf(x),
            "f_first": bf(np.random.standard_normal((NK, NK, 2, 2, C, CM)) * np.sqrt(0.5 / C) / s[:, :, :, None] * t),
            "b_first": bf(np.random.standard_normal((NK, NK, CM)) * 0.2 * t),
            "f_second": bf(np.random.standard_normal((NK, NK, 2, 2, CM, CO)) * np.sqrt(0.5 / CM) / t[:, None]),
            "b_second": bf(np.random.standard_normal((NK, NK, CO)) * 0.2)}


def reference(x_leaf, f_first, b_first, f_second, b_second):
    h = node_conv(f64(x_leaf), f64(f_first), f64(b_first))
    return node_conv(h, f64(f_second), f64(b_second))

@@ -1,0 +1,173 @@
+from contextlib import ExitStack
+
+import concourse.mybir as mybir
+from concourse.masks import make_identity
+
+F32 = mybir.dt.float32
+BF16 = mybir.dt.bfloat16
+I32 = mybir.dt.int32
+U32 = mybir.dt.uint32
+U8 = mybir.dt.uint8
+FP8X4 = mybir.dt.float8_e4m3fn_x4
+RELU = mybir.ActivationFunctionType.Relu
+ADD = mybir.AluOpType.add
+
+P = 128
+PACK = 4
+NODES = 16
+CH = 128
+ROWS1 = 32
+ROWS2 = 8
+CHUNK = 4
+CHUNKS = NODES // CHUNK
+DIAG = CH + ROWS2
+
+FLOPS = 2 * NODES * (ROWS1 + ROWS2) * (PACK * CH) * CH
+
+
+def quantise_weight_chunk(nc, raw, grouped, codes, scales):
+    for n in range(CHUNK):
+        src = raw[:, n].rearrange("p t (c i) -> p c t i", i=4)
+        dst = grouped[:, n].rearrange("p (c i) t -> p c t i", i=4)
+        if n < CHUNK // 2:
+            nc.vector.tensor_copy(out=dst, in_=src)
+        else:
+            nc.scalar.copy(out=dst, in_=src)
+    nc.vector.quantize_mx(
+        out=codes.bitcast(FP8X4),
+        scales=scales,
+        in_=grouped[:].rearrange("p n o t -> p (n o t)"),
+    )
+
+
+def tile_butterflylayer2d_pb_s_kernel(tc, x_leaf, f_first, b_first, f_second, b_second, out):
+    nc = tc.nc
+    with ExitStack() as ctx:
+        keep = ctx.enter_context(tc.tile_pool(name="keep", bufs=1))
+        psum = ctx.enter_context(tc.psum_pool(name="psum", bufs=1))
+
+        x_sb = keep.tile([P, 4 * PACK * CH], BF16)
+        x_rows = x_leaf.rearrange("a b n (y p) (x q) c -> p (a b n y) x (q c)", p=2, q=2)
+        x_dst = x_sb[:].rearrange("r (x p w) -> r x p w", x=4, p=2)
+        for p in range(2):
+            nc.sync.dma_start(out=x_dst[:, :, p, :], in_=x_rows[p])
+
+        w1_rows = f_first.rearrange("a b p q (c t) o -> (p q c) (a b) t o", t=PACK)
+        w2_rows = f_second.rearrange("a b p q c o -> c (a b) (p q) o")
+        raw = {}
+        for level, rows in ((1, w1_rows), (2, w2_rows)):
+            for c in range(CHUNKS):
+                raw[level, c] = keep.tile([P, CHUNK, PACK, CH], BF16, name="raw_%d_%d" % (level, c))
+                nc.sync.dma_start(out=raw[level, c][:], in_=rows[:, c * CHUNK : (c + 1) * CHUNK])
+
+        ident_f32 = keep.tile([P, P], F32)
+        make_identity(nc, ident_f32[:])
+        ident_bf16 = keep.tile([P, P], BF16)
+        make_identity(nc, ident_bf16[:])
+
+        b1_rows = keep.tile([P, CH], BF16)
+        nc.vector.memset(b1_rows[:], 0.0)
+        nc.scalar.dma_start(out=b1_rows[0:NODES, :], in_=b_first.rearrange("a b o -> (a b) o"))
+        b2_rep = keep.tile([P, CH], BF16)
+        for r in range(ROWS2):
+            nc.gpsimd.dma_start(out=b2_rep[r:P:ROWS2, :], in_=b_second.rearrange("a b o -> (a b) o"))
+
+        h_diag_codes = keep.tile([P, NODES * DIAG], U32, align_bytes=64)
+        h_diag_scales = keep.tile([P, NODES * DIAG], U8, align_bytes=64)
+        h_scales = keep.tile([P, NODES * ROWS2], U8, align_bytes=64)
+        nc.vector.memset(h_diag_codes[:].bitcast(I32), 0)
+        nc.vector.memset(h_diag_scales[:].bitcast(I32), 0)
+        nc.vector.memset(h_scales[:].bitcast(I32), 0)
+
+        b1_t_ps = psum.tile([P, P], BF16)
+        nc.tensor.transpose(b1_t_ps[:], b1_rows[:], ident_bf16[:])
+        b1_t = keep.tile([P, NODES], F32)
+        nc.vector.tensor_copy(out=b1_t[:], in_=b1_t_ps[:, 0:NODES])
+
+        x_words = x_sb[:].bitcast(F32).rearrange("r (x k u) -> r x k u", x=4, u=2)
+        grouped_x = keep.tile([P, NODES * ROWS1 * PACK], BF16, align_bytes=64)
+        gx_words = grouped_x[:].bitcast(F32).rearrange(
+            "k (m x s q u) -> k x m s q u", x=2, s=2, q=2, u=2
+        )
+        for x2 in range(2):
+            xt = psum.tile([P, 2, 2, P], F32, name="xt_%d" % x2)
+            for q2 in range(2):
+                for u in range(2):
+                    nc.tensor.transpose(xt[:, q2, u, :], x_words[:, 2 * x2 + q2, :, u], ident_f32[:])
+            xt_view = xt[:].rearrange("k q u (m s) -> k m s q u", s=2)
+            if x2 == 0:
+                nc.vector.tensor_copy(out=gx_words[:, x2], in_=xt_view)
+            else:
+                nc.scalar.copy(out=gx_words[:, x2], in_=xt_view)
+        x_codes = keep.tile([P, NODES * ROWS1], U32, align_bytes=64)
+        x_scales = keep.tile([P, NODES * ROWS1], U8, align_bytes=64)
+        nc.vector.quantize_mx(out=x_codes[:].bitcast(FP8X4), scales=x_scales[:], in_=grouped_x[:])
+
+        w_codes = {}
+        w_scales = {}
+        for level in (1, 2):
+            w_codes[level] = keep.tile([P, NODES * CH], U32, name="w_codes_%d" % level, align_bytes=64)
+            w_scales[level] = keep.tile([P, NODES * CH], U8, name="w_scales_%d" % level, align_bytes=64)
+
+        grouped_h = keep.tile([P, NODES * ROWS1], BF16, align_bytes=64)
+        for c in range(CHUNKS):
+            cols = slice(c * CHUNK * CH, (c + 1) * CHUNK * CH)
+            grouped = keep.tile([P, CHUNK, CH, PACK], BF16, name="grouped_1_%d" % c, align_bytes=64)
+            quantise_weight_chunk(nc, raw[1, c], grouped, w_codes[1][:, cols], w_scales[1][:, cols])
+            x_cols = slice(c * CHUNK * ROWS1, (c + 1) * CHUNK * ROWS1)
+            h_ps = psum.tile([P, CHUNK, CHUNK * ROWS1], F32, name="h_ps_%d" % c)
+            for n in range(CHUNK):
+                node = c * CHUNK + n
+                o_cols = slice(node * CH, (node + 1) * CH)
+                nc.tensor.matmul_mx(
+                    out=h_ps[:, n, :],
+                    lhsT=w_codes[1][:, o_cols].bitcast(FP8X4),
+                    lhsT_scale=w_scales[1][:, o_cols],
+                    rhs=x_codes[:, x_cols].bitcast(FP8X4),
+                    rhs_scale=x_scales[:, x_cols],
+                    start=True,
+                    stop=True,
+                )
+            for n in range(CHUNK):
+                node = c * CHUNK + n
+                nc.scalar.activation(
+                    out=grouped_h[:, node * ROWS1 : (node + 1) * ROWS1],
+                    in_=h_ps[:, n, n * ROWS1 : (n + 1) * ROWS1],
+                    func=RELU,
+                    bias=b1_t[:, node : node + 1],
+                )
+
+        h_codes = keep.tile([P, NODES * ROWS2], U32, align_bytes=64)
+        nc.vector.quantize_mx(out=h_codes[:].bitcast(FP8X4), scales=h_scales[:], in_=grouped_h[:])
+        nc.vector.tensor_copy(
+            out=h_diag_codes[:].bitcast(I32).rearrange("k (i s) -> k i s", s=DIAG)[:, :, 0:ROWS2],
+            in_=h_codes[:].bitcast(I32).rearrange("k (i s) -> k i s", s=ROWS2),
+        )
+        nc.vector.tensor_copy(
+            out=h_diag_scales[:].bitcast(I32).rearrange("k (i s) -> k i s", s=DIAG // 4)[:, :, 0 : ROWS2 // 4],
+            in_=h_scales[:].bitcast(I32).rearrange("k (i s) -> k i s", s=ROWS2 // 4),
+        )
+
+        out_ps = psum.tile([P, CH], F32)
+        for c in range(CHUNKS):
+            cols = slice(c * CHUNK * CH, (c + 1) * CHUNK * CH)
+            grouped = keep.tile([P, CHUNK, CH, PACK], BF16, name="grouped_2_%d" % c, align_bytes=64)
+            quantise_weight_chunk(nc, raw[2, c], grouped, w_codes[2][:, cols], w_scales[2][:, cols])
+            for n in range(CHUNK):
+                node = c * CHUNK + n
+                o_cols = slice(node * CH, (node + 1) * CH)
+                nc.tensor.matmul_mx(
+                    out=out_ps[:],
+                    lhsT=h_diag_codes[:, o_cols].bitcast(FP8X4),
+                    lhsT_scale=h_diag_scales[:, o_cols],
+                    rhs=w_codes[2][:, o_cols].bitcast(FP8X4),
+                    rhs_scale=w_scales[2][:, o_cols],
+                    start=(node == 0),
+                    stop=(node == NODES - 1),
+                )
+
+        biased = keep.tile([P, CH], F32)
+        nc.vector.tensor_tensor(out=biased[:], in0=out_ps[:], in1=b2_rep[:], op=ADD)
+        result = keep.tile([P, CH], F32)
+        nc.vector.tensor_scalar_max(out=result[:], in0=biased[:], scalar1=0.0)
+        nc.sync.dma_start(out=out.rearrange("a b n y x o -> (a b n y x) o"), in_=result[:])

@@ -18,25 +18,21 @@ NODES = 16
 CH = 128
 ROWS1 = 32
 ROWS2 = 8
-CHUNK = 4
-CHUNKS = NODES // CHUNK
+WINDOW = 4
 DIAG = CH + ROWS2
 
 FLOPS = 2 * NODES * (ROWS1 + ROWS2) * (PACK * CH) * CH
 
+UNITS_1 = [(1, n, 2) for n in range(0, NODES, 2)]
+UNITS_2 = [(2, n, 2) for n in range(0, NODES - 2, 2)] + [(2, NODES - 2, 1), (2, NODES - 1, 1)]
+UNITS = UNITS_1 + UNITS_2
+VECTOR_COLS = 80
 
-def quantise_weight_chunk(nc, raw, grouped, codes, scales):
-    for n in range(CHUNK):
-        src = raw[:, n].rearrange("p t (c i) -> p c t i", i=4)
-        dst = grouped[:, n].rearrange("p (c i) t -> p c t i", i=4)
-        if n < CHUNK // 2:
-            nc.vector.tensor_copy(out=dst, in_=src)
-        else:
-            nc.scalar.copy(out=dst, in_=src)
-    nc.vector.quantize_mx(
-        out=codes.bitcast(FP8X4),
-        scales=scales,
-        in_=grouped[:].rearrange("p n o t -> p (n o t)"),
+
+def regroup(copy, raw, grouped, n, o0, o1):
+    copy(
+        out=grouped[:, n, o0:o1].rearrange("p (c i) t -> p c t i", i=4),
+        in_=raw[:, n, :, o0:o1].rearrange("p t (c i) -> p c t i", i=4),
     )
 
 
@@ -45,129 +41,195 @@ def tile_butterflylayer2d_pb_s_kernel(tc, x_leaf, f_first, b_first, f_second, b_
     with ExitStack() as ctx:
         keep = ctx.enter_context(tc.tile_pool(name="keep", bufs=1))
         psum = ctx.enter_context(tc.psum_pool(name="psum", bufs=1))
+        ctx.enter_context(tc.manual_schedule())
+
+        w_rows = {
+            1: f_first.rearrange("a b p q (c t) o -> (p q c) (a b) t o", t=PACK),
+            2: f_second.rearrange("a b p q c o -> c (a b) (p q) o"),
+        }
+        raw = []
+        for u, (level, node, count) in enumerate(UNITS):
+            raw.append(keep.tile([P, count, PACK, CH], BF16, name="raw_%d" % u))
+
+        def load(u):
+            level, node, count = UNITS[u]
+            nc.sync.dma_start(out=raw[u][:], in_=w_rows[level][:, node : node + count])
 
         x_sb = keep.tile([P, 4 * PACK * CH], BF16)
         x_rows = x_leaf.rearrange("a b n (y p) (x q) c -> p (a b n y) x (q c)", p=2, q=2)
         x_dst = x_sb[:].rearrange("r (x p w) -> r x p w", x=4, p=2)
+
+        b_rows = keep.tile([P, CH], BF16)
+        nc.vector.memset(b_rows[:], 0.0)
+        load(0)
         for p in range(2):
             nc.sync.dma_start(out=x_dst[:, :, p, :], in_=x_rows[p])
-
-        w1_rows = f_first.rearrange("a b p q (c t) o -> (p q c) (a b) t o", t=PACK)
-        w2_rows = f_second.rearrange("a b p q c o -> c (a b) (p q) o")
-        raw = {}
-        for level, rows in ((1, w1_rows), (2, w2_rows)):
-            for c in range(CHUNKS):
-                raw[level, c] = keep.tile([P, CHUNK, PACK, CH], BF16, name="raw_%d_%d" % (level, c))
-                nc.sync.dma_start(out=raw[level, c][:], in_=rows[:, c * CHUNK : (c + 1) * CHUNK])
+        for u in range(1, len(UNITS)):
+            load(u)
+        nc.scalar.dma_start(out=b_rows[0:NODES, :], in_=b_first.rearrange("a b o -> (a b) o"))
+        nc.scalar.dma_start(out=b_rows[NODES : 2 * NODES, :], in_=b_second.rearrange("a b o -> (a b) o"))
 
         ident_f32 = keep.tile([P, P], F32)
         make_identity(nc, ident_f32[:])
         ident_bf16 = keep.tile([P, P], BF16)
         make_identity(nc, ident_bf16[:])
 
-        b1_rows = keep.tile([P, CH], BF16)
-        nc.vector.memset(b1_rows[:], 0.0)
-        nc.scalar.dma_start(out=b1_rows[0:NODES, :], in_=b_first.rearrange("a b o -> (a b) o"))
-        b2_rep = keep.tile([P, CH], BF16)
-        for r in range(ROWS2):
-            nc.gpsimd.dma_start(out=b2_rep[r:P:ROWS2, :], in_=b_second.rearrange("a b o -> (a b) o"))
+        h_diag = keep.tile([P, NODES * DIAG], U32, align_bytes=64)
+        nc.vector.memset(h_diag[:].bitcast(I32), 0)
 
-        h_diag_codes = keep.tile([P, NODES * DIAG], U32, align_bytes=64)
-        h_diag_scales = keep.tile([P, NODES * DIAG], U8, align_bytes=64)
-        h_scales = keep.tile([P, NODES * ROWS2], U8, align_bytes=64)
-        nc.vector.memset(h_diag_codes[:].bitcast(I32), 0)
-        nc.vector.memset(h_diag_scales[:].bitcast(I32), 0)
-        nc.vector.memset(h_scales[:].bitcast(I32), 0)
+        spread = keep.tile([P, NODES, ROWS2], BF16)
+        nc.vector.tensor_copy(
+            out=spread[:], in_=ident_bf16[:, NODES : 2 * NODES].unsqueeze(2).to_broadcast([P, NODES, ROWS2])
+        )
 
-        b1_t_ps = psum.tile([P, P], BF16)
-        nc.tensor.transpose(b1_t_ps[:], b1_rows[:], ident_bf16[:])
-        b1_t = keep.tile([P, NODES], F32)
-        nc.vector.tensor_copy(out=b1_t[:], in_=b1_t_ps[:, 0:NODES])
+        grouped = []
+        w_codes = []
+        w_scales = []
+        for u, (level, node, count) in enumerate(UNITS):
+            grouped.append(keep.tile([P, count, CH, PACK], BF16, name="grouped_%d" % u, align_bytes=64))
+            w_codes.append(keep.tile([P, count * CH], U32, name="w_codes_%d" % u, align_bytes=64))
+            w_scales.append(keep.tile([P, count * CH], U8, name="w_scales_%d" % u, align_bytes=64))
+
+        def copy(u):
+            if UNITS[u][2] == 2:
+                regroup(nc.vector.tensor_copy, raw[u], grouped[u], 0, 0, CH)
+                regroup(nc.scalar.copy, raw[u], grouped[u], 1, 0, CH)
+            else:
+                regroup(nc.vector.tensor_copy, raw[u], grouped[u], 0, 0, VECTOR_COLS)
+                regroup(nc.scalar.copy, raw[u], grouped[u], 0, VECTOR_COLS, CH)
+
+        def quantise(u):
+            nc.vector.quantize_mx(
+                out=w_codes[u][:].bitcast(FP8X4),
+                scales=w_scales[u][:],
+                in_=grouped[u][:].rearrange("p n o t -> p (n o t)"),
+            )
 
         x_words = x_sb[:].bitcast(F32).rearrange("r (x k u) -> r x k u", x=4, u=2)
         grouped_x = keep.tile([P, NODES * ROWS1 * PACK], BF16, align_bytes=64)
-        gx_words = grouped_x[:].bitcast(F32).rearrange(
-            "k (m x s q u) -> k x m s q u", x=2, s=2, q=2, u=2
-        )
-        for x2 in range(2):
-            xt = psum.tile([P, 2, 2, P], F32, name="xt_%d" % x2)
-            for q2 in range(2):
-                for u in range(2):
-                    nc.tensor.transpose(xt[:, q2, u, :], x_words[:, 2 * x2 + q2, :, u], ident_f32[:])
-            xt_view = xt[:].rearrange("k q u (m s) -> k m s q u", s=2)
-            if x2 == 0:
-                nc.vector.tensor_copy(out=gx_words[:, x2], in_=xt_view)
-            else:
-                nc.scalar.copy(out=gx_words[:, x2], in_=xt_view)
+        gx_words = grouped_x[:].bitcast(F32).rearrange("k (m x s q u) -> k x m s q u", x=2, s=2, q=2, u=2)
         x_codes = keep.tile([P, NODES * ROWS1], U32, align_bytes=64)
         x_scales = keep.tile([P, NODES * ROWS1], U8, align_bytes=64)
-        nc.vector.quantize_mx(out=x_codes[:].bitcast(FP8X4), scales=x_scales[:], in_=grouped_x[:])
 
-        w_codes = {}
-        w_scales = {}
-        for level in (1, 2):
-            w_codes[level] = keep.tile([P, NODES * CH], U32, name="w_codes_%d" % level, align_bytes=64)
-            w_scales[level] = keep.tile([P, NODES * CH], U8, name="w_scales_%d" % level, align_bytes=64)
+        def turn_x():
+            for x2 in range(2):
+                xt = psum.tile([P, 2, 2, P], F32, name="xt_%d" % x2)
+                for q2 in range(2):
+                    for u in range(2):
+                        nc.tensor.transpose(xt[:, q2, u, :], x_words[:, 2 * x2 + q2, :, u], ident_f32[:])
+                xt_view = xt[:].rearrange("k q u (m s) -> k m s q u", s=2)
+                if x2 == 0:
+                    nc.vector.tensor_copy(out=gx_words[:, x2], in_=xt_view)
+                else:
+                    nc.scalar.copy(out=gx_words[:, x2], in_=xt_view)
+
+        def quantise_x():
+            nc.vector.quantize_mx(out=x_codes[:].bitcast(FP8X4), scales=x_scales[:], in_=grouped_x[:])
+
+        b1_t = keep.tile([P, NODES], F32)
+        b2_rep = keep.tile([P, CH], F32)
+
+        def biases():
+            b1_ps = psum.tile([P, P], BF16)
+            nc.tensor.transpose(b1_ps[:], b_rows[:], ident_bf16[:])
+            b2_ps = psum.tile([P, CH], F32)
+            nc.tensor.matmul(
+                b2_ps[:], lhsT=spread[:].rearrange("p n r -> p (n r)"), rhs=b_rows[:], start=True, stop=True
+            )
+            nc.scalar.copy(out=b1_t[:], in_=b1_ps[:, 0:NODES])
+            nc.scalar.copy(out=b2_rep[:], in_=b2_ps[:])
 
         grouped_h = keep.tile([P, NODES * ROWS1], BF16, align_bytes=64)
-        for c in range(CHUNKS):
-            cols = slice(c * CHUNK * CH, (c + 1) * CHUNK * CH)
-            grouped = keep.tile([P, CHUNK, CH, PACK], BF16, name="grouped_1_%d" % c, align_bytes=64)
-            quantise_weight_chunk(nc, raw[1, c], grouped, w_codes[1][:, cols], w_scales[1][:, cols])
-            x_cols = slice(c * CHUNK * ROWS1, (c + 1) * CHUNK * ROWS1)
-            h_ps = psum.tile([P, CHUNK, CHUNK * ROWS1], F32, name="h_ps_%d" % c)
-            for n in range(CHUNK):
-                node = c * CHUNK + n
-                o_cols = slice(node * CH, (node + 1) * CH)
+        h_ps = {}
+
+        def multiply_1(u):
+            level, first, count = UNITS[u]
+            for n in range(count):
+                node = first + n
+                c = node // WINDOW
+                if node % WINDOW == 0:
+                    h_ps[c] = psum.tile([P, WINDOW, WINDOW * ROWS1], F32, name="h_ps_%d" % (c % 2))
+                x_cols = slice(c * WINDOW * ROWS1, (c + 1) * WINDOW * ROWS1)
+                o_cols = slice(n * CH, (n + 1) * CH)
                 nc.tensor.matmul_mx(
-                    out=h_ps[:, n, :],
-                    lhsT=w_codes[1][:, o_cols].bitcast(FP8X4),
-                    lhsT_scale=w_scales[1][:, o_cols],
+                    out=h_ps[c][:, node % WINDOW, :],
+                    lhsT=w_codes[u][:, o_cols].bitcast(FP8X4),
+                    lhsT_scale=w_scales[u][:, o_cols],
                     rhs=x_codes[:, x_cols].bitcast(FP8X4),
                     rhs_scale=x_scales[:, x_cols],
                     start=True,
                     stop=True,
                 )
-            for n in range(CHUNK):
-                node = c * CHUNK + n
+
+        def finish_1(u):
+            level, first, count = UNITS[u]
+            for node in range(first, first + count):
+                n = node % WINDOW
                 nc.scalar.activation(
                     out=grouped_h[:, node * ROWS1 : (node + 1) * ROWS1],
-                    in_=h_ps[:, n, n * ROWS1 : (n + 1) * ROWS1],
+                    in_=h_ps[node // WINDOW][:, n, n * ROWS1 : (n + 1) * ROWS1],
                     func=RELU,
                     bias=b1_t[:, node : node + 1],
                 )
 
         h_codes = keep.tile([P, NODES * ROWS2], U32, align_bytes=64)
-        nc.vector.quantize_mx(out=h_codes[:].bitcast(FP8X4), scales=h_scales[:], in_=grouped_h[:])
-        nc.vector.tensor_copy(
-            out=h_diag_codes[:].bitcast(I32).rearrange("k (i s) -> k i s", s=DIAG)[:, :, 0:ROWS2],
-            in_=h_codes[:].bitcast(I32).rearrange("k (i s) -> k i s", s=ROWS2),
-        )
-        nc.vector.tensor_copy(
-            out=h_diag_scales[:].bitcast(I32).rearrange("k (i s) -> k i s", s=DIAG // 4)[:, :, 0 : ROWS2 // 4],
-            in_=h_scales[:].bitcast(I32).rearrange("k (i s) -> k i s", s=ROWS2 // 4),
-        )
+        h_scales = keep.tile([P, NODES * ROWS2], U8, align_bytes=64)
+
+        def quantise_h():
+            nc.vector.quantize_mx(out=h_codes[:].bitcast(FP8X4), scales=h_scales[:], in_=grouped_h[:])
+
+        def spread_h():
+            nc.vector.tensor_copy(
+                out=h_diag[:].bitcast(I32).rearrange("k (i s) -> k i s", s=DIAG)[:, :, 0:ROWS2],
+                in_=h_codes[:].bitcast(I32).rearrange("k (i s) -> k i s", s=ROWS2),
+            )
 
         out_ps = psum.tile([P, CH], F32)
-        for c in range(CHUNKS):
-            cols = slice(c * CHUNK * CH, (c + 1) * CHUNK * CH)
-            grouped = keep.tile([P, CHUNK, CH, PACK], BF16, name="grouped_2_%d" % c, align_bytes=64)
-            quantise_weight_chunk(nc, raw[2, c], grouped, w_codes[2][:, cols], w_scales[2][:, cols])
-            for n in range(CHUNK):
-                node = c * CHUNK + n
-                o_cols = slice(node * CH, (node + 1) * CH)
+
+        def multiply_2(u):
+            level, first, count = UNITS[u]
+            for n in range(count):
+                node = first + n
+                o_cols = slice(n * CH, (n + 1) * CH)
                 nc.tensor.matmul_mx(
                     out=out_ps[:],
-                    lhsT=h_diag_codes[:, o_cols].bitcast(FP8X4),
-                    lhsT_scale=h_diag_scales[:, o_cols],
-                    rhs=w_codes[2][:, o_cols].bitcast(FP8X4),
-                    rhs_scale=w_scales[2][:, o_cols],
+                    lhsT=h_diag[:, node * CH : (node + 1) * CH].bitcast(FP8X4),
+                    lhsT_scale=h_scales[:],
+                    rhs=w_codes[u][:, o_cols].bitcast(FP8X4),
+                    rhs_scale=w_scales[u][:, o_cols],
                     start=(node == 0),
                     stop=(node == NODES - 1),
                 )
 
+        n1 = len(UNITS_1)
+        copy(0)
+        quantise(0)
+        copy(1)
+        turn_x()
+        biases()
+        quantise(1)
+        quantise_x()
+        multiply_1(0)
+        for u in range(2, len(UNITS)):
+            copy(u)
+            if 0 <= u - 2 < n1:
+                finish_1(u - 2)
+            quantise(u - 1)
+            if u - 1 < n1:
+                multiply_1(u - 1)
+            if u == n1 + 2:
+                quantise_h()
+            if u == n1 + 3:
+                spread_h()
+                for v in range(n1, u):
+                    multiply_2(v)
+            if u > n1 + 3:
+                multiply_2(u - 1)
+        quantise(len(UNITS) - 1)
+        multiply_2(len(UNITS) - 1)
+
         biased = keep.tile([P, CH], F32)
         nc.vector.tensor_tensor(out=biased[:], in0=out_ps[:], in1=b2_rep[:], op=ADD)
         result = keep.tile([P, CH], F32)
-        nc.vector.tensor_scalar_max(out=result[:], in0=biased[:], scalar1=0.0)
+        nc.scalar.activation(out=result[:], in_=biased[:], func=RELU)
         nc.sync.dma_start(out=out.rearrange("a b n y x o -> (a b n y x) o"), in_=result[:])

@@ -44,8 +44,8 @@ def tile_butterflylayer2d_pb_s_kernel(tc, x_leaf, f_first, b_first, f_second, b_
         ctx.enter_context(tc.manual_schedule())
 
         w_rows = {
-            1: f_first.rearrange("a b p q (c t) o -> (p q c) (a b) t o", t=PACK),
-            2: f_second.rearrange("a b p q c o -> c (a b) (p q) o"),
+            level: f.rearrange("a b p q (c t) o -> (p q c) (a b) t o", t=PACK)
+            for level, f in ((1, f_first), (2, f_second))
         }
         raw = []
         for u, (level, node, count) in enumerate(UNITS):
@@ -61,10 +61,11 @@ def tile_butterflylayer2d_pb_s_kernel(tc, x_leaf, f_first, b_first, f_second, b_
 
         b_rows = keep.tile([P, CH], BF16)
         nc.vector.memset(b_rows[:], 0.0)
-        load(0)
+        for u in range(2):
+            load(u)
         for p in range(2):
             nc.sync.dma_start(out=x_dst[:, :, p, :], in_=x_rows[p])
-        for u in range(1, len(UNITS)):
+        for u in range(2, len(UNITS)):
             load(u)
         nc.scalar.dma_start(out=b_rows[0:NODES, :], in_=b_first.rearrange("a b o -> (a b) o"))
         nc.scalar.dma_start(out=b_rows[NODES : 2 * NODES, :], in_=b_second.rearrange("a b o -> (a b) o"))
@@ -113,7 +114,7 @@ def tile_butterflylayer2d_pb_s_kernel(tc, x_leaf, f_first, b_first, f_second, b_
 
         def turn_x():
             for x2 in range(2):
-                xt = psum.tile([P, 2, 2, P], F32, name="xt_%d" % x2)
+                xt = psum.tile([P, 2, 2, P], F32, name="turn_%d" % x2)
                 for q2 in range(2):
                     for u in range(2):
                         nc.tensor.transpose(xt[:, q2, u, :], x_words[:, 2 * x2 + q2, :, u], ident_f32[:])
@@ -129,17 +130,19 @@ def tile_butterflylayer2d_pb_s_kernel(tc, x_leaf, f_first, b_first, f_second, b_
         b1_t = keep.tile([P, NODES], F32)
         b2_rep = keep.tile([P, CH], F32)
 
-        def biases():
+        def bias_1():
             b1_ps = psum.tile([P, P], BF16)
             nc.tensor.transpose(b1_ps[:], b_rows[:], ident_bf16[:])
+            nc.scalar.copy(out=b1_t[:], in_=b1_ps[:, 0:NODES])
+
+        def bias_2():
             b2_ps = psum.tile([P, CH], F32)
             nc.tensor.matmul(
                 b2_ps[:], lhsT=spread[:].rearrange("p n r -> p (n r)"), rhs=b_rows[:], start=True, stop=True
             )
-            nc.scalar.copy(out=b1_t[:], in_=b1_ps[:, 0:NODES])
             nc.scalar.copy(out=b2_rep[:], in_=b2_ps[:])
 
-        grouped_h = keep.tile([P, NODES * ROWS1], BF16, align_bytes=64)
+        h_by_channel = keep.tile([P, NODES * ROWS2, PACK], BF16)
         h_ps = {}
 
         def multiply_1(u):
@@ -166,11 +169,30 @@ def tile_butterflylayer2d_pb_s_kernel(tc, x_leaf, f_first, b_first, f_second, b_
             for node in range(first, first + count):
                 n = node % WINDOW
                 nc.scalar.activation(
-                    out=grouped_h[:, node * ROWS1 : (node + 1) * ROWS1],
+                    out=h_by_channel[:, node * ROWS2 : (node + 1) * ROWS2].rearrange("c m t -> c (m t)"),
                     in_=h_ps[node // WINDOW][:, n, n * ROWS1 : (n + 1) * ROWS1],
                     func=RELU,
                     bias=b1_t[:, node : node + 1],
                 )
+
+        h_by_pixel = keep.tile([P, PACK * CH], BF16)
+        grouped_h = keep.tile([P, NODES * ROWS2 * PACK], BF16, align_bytes=64)
+
+        def turn_h_to_pixels():
+            turned = psum.tile([P, PACK, CH], BF16, name="turn_0")
+            for place in range(PACK):
+                nc.tensor.transpose(turned[:, place, :], h_by_channel[:, :, place], ident_bf16[:])
+            nc.vector.tensor_copy(out=h_by_pixel[:], in_=turned[:].rearrange("m t o -> m (t o)"))
+
+        def turn_h_to_k():
+            words = h_by_pixel[:].bitcast(F32).rearrange("m (k u) -> m k u", u=2)
+            turned = psum.tile([P, 2, P], F32, name="turn_1")
+            for u in range(2):
+                nc.tensor.transpose(turned[:, u, :], words[:, :, u], ident_f32[:])
+            nc.scalar.copy(
+                out=grouped_h[:].bitcast(F32).rearrange("k (m u) -> k m u", u=2),
+                in_=turned[:].rearrange("k u m -> k m u"),
+            )
 
         h_codes = keep.tile([P, NODES * ROWS2], U32, align_bytes=64)
         h_scales = keep.tile([P, NODES * ROWS2], U8, align_bytes=64)
@@ -203,27 +225,44 @@ def tile_butterflylayer2d_pb_s_kernel(tc, x_leaf, f_first, b_first, f_second, b_
 
         n1 = len(UNITS_1)
         copy(0)
-        quantise(0)
         copy(1)
-        turn_x()
-        biases()
+        quantise(0)
+        copy(2)
         quantise(1)
+        turn_x()
+        bias_1()
+        copy(3)
+        quantise(2)
         quantise_x()
-        multiply_1(0)
-        for u in range(2, len(UNITS)):
+        for u in range(3):
+            multiply_1(u)
+        for u in range(4, len(UNITS)):
             copy(u)
-            if 0 <= u - 2 < n1:
+            if u == 4:
+                finish_1(0)
+            elif u == 5:
+                finish_1(1)
+                finish_1(2)
+            elif u == 6:
+                finish_1(3)
+                finish_1(4)
+            elif u - 2 < n1:
                 finish_1(u - 2)
             quantise(u - 1)
             if u - 1 < n1:
                 multiply_1(u - 1)
             if u == n1 + 2:
-                quantise_h()
+                turn_h_to_pixels()
+                bias_2()
             if u == n1 + 3:
+                turn_h_to_k()
+            if u == n1 + 4:
+                quantise_h()
+            if u == n1 + 5:
                 spread_h()
                 for v in range(n1, u):
                     multiply_2(v)
-            if u > n1 + 3:
+            if u > n1 + 5:
                 multiply_2(u - 1)
         quantise(len(UNITS) - 1)
         multiply_2(len(UNITS) - 1)

@@ -23,16 +23,16 @@ DIAG = CH + ROWS2
 
 FLOPS = 2 * NODES * (ROWS1 + ROWS2) * (PACK * CH) * CH
 
-UNITS_1 = [(1, n, 2) for n in range(0, NODES, 2)]
-UNITS_2 = [(2, n, 2) for n in range(0, NODES - 2, 2)] + [(2, NODES - 2, 1), (2, NODES - 1, 1)]
+UNITS_1 = [(1, 0, 2), (1, 2, 2), (1, 4, 2), (1, 6, 2), (1, 8, 4), (1, 12, 4)]
+UNITS_2 = [(2, 0, 4), (2, 4, 4), (2, 8, 4), (2, 12, 2), (2, 14, 1), (2, 15, 1)]
 UNITS = UNITS_1 + UNITS_2
-VECTOR_COLS = 80
+VECTOR_COLS = 72
 
 
-def regroup(copy, raw, grouped, n, o0, o1):
+def regroup(copy, raw, grouped, o0, o1):
     copy(
-        out=grouped[:, n, o0:o1].rearrange("p (c i) t -> p c t i", i=4),
-        in_=raw[:, n, :, o0:o1].rearrange("p t (c i) -> p c t i", i=4),
+        out=grouped[:, :, o0:o1].rearrange("p n (c i) t -> p n c t i", i=4),
+        in_=raw[:, :, :, o0:o1].rearrange("p n t (c i) -> p n c t i", i=4),
     )
 
 
@@ -56,19 +56,19 @@ def tile_butterflylayer2d_pb_s_kernel(tc, x_leaf, f_first, b_first, f_second, b_
             nc.sync.dma_start(out=raw[u][:], in_=w_rows[level][:, node : node + count])
 
         x_sb = keep.tile([P, 4 * PACK * CH], BF16)
-        x_rows = x_leaf.rearrange("a b n (y p) (x q) c -> p (a b n y) x (q c)", p=2, q=2)
+        x_rows = x_leaf.rearrange("a b n (y p) (x q) c -> x (a b n y) p (q c)", p=2, q=2)
         x_dst = x_sb[:].rearrange("r (x p w) -> r x p w", x=4, p=2)
 
         b_rows = keep.tile([P, CH], BF16)
         nc.vector.memset(b_rows[:], 0.0)
-        for u in range(2):
+        for u in range(4):
             load(u)
-        for p in range(2):
-            nc.sync.dma_start(out=x_dst[:, :, p, :], in_=x_rows[p])
-        for u in range(2, len(UNITS)):
+        for x in range(4):
+            nc.sync.dma_start(out=x_dst[:, x], in_=x_rows[x])
+        nc.sync.dma_start(out=b_rows[0:NODES, :], in_=b_first.rearrange("a b o -> (a b) o"))
+        nc.sync.dma_start(out=b_rows[NODES : 2 * NODES, :], in_=b_second.rearrange("a b o -> (a b) o"))
+        for u in range(4, len(UNITS)):
             load(u)
-        nc.scalar.dma_start(out=b_rows[0:NODES, :], in_=b_first.rearrange("a b o -> (a b) o"))
-        nc.scalar.dma_start(out=b_rows[NODES : 2 * NODES, :], in_=b_second.rearrange("a b o -> (a b) o"))
 
         ident_f32 = keep.tile([P, P], F32)
         make_identity(nc, ident_f32[:])
@@ -91,13 +91,15 @@ def tile_butterflylayer2d_pb_s_kernel(tc, x_leaf, f_first, b_first, f_second, b_
             w_codes.append(keep.tile([P, count * CH], U32, name="w_codes_%d" % u, align_bytes=64))
             w_scales.append(keep.tile([P, count * CH], U8, name="w_scales_%d" % u, align_bytes=64))
 
+        def copy_vector(u):
+            regroup(nc.vector.tensor_copy, raw[u], grouped[u], 0, VECTOR_COLS)
+
+        def copy_scalar(u):
+            regroup(nc.scalar.copy, raw[u], grouped[u], VECTOR_COLS, CH)
+
         def copy(u):
-            if UNITS[u][2] == 2:
-                regroup(nc.vector.tensor_copy, raw[u], grouped[u], 0, 0, CH)
-                regroup(nc.scalar.copy, raw[u], grouped[u], 1, 0, CH)
-            else:
-                regroup(nc.vector.tensor_copy, raw[u], grouped[u], 0, 0, VECTOR_COLS)
-                regroup(nc.scalar.copy, raw[u], grouped[u], 0, VECTOR_COLS, CH)
+            copy_vector(u)
+            copy_scalar(u)
 
         def quantise(u):
             nc.vector.quantize_mx(
@@ -112,17 +114,16 @@ def tile_butterflylayer2d_pb_s_kernel(tc, x_leaf, f_first, b_first, f_second, b_
         x_codes = keep.tile([P, NODES * ROWS1], U32, align_bytes=64)
         x_scales = keep.tile([P, NODES * ROWS1], U8, align_bytes=64)
 
-        def turn_x():
-            for x2 in range(2):
-                xt = psum.tile([P, 2, 2, P], F32, name="turn_%d" % x2)
-                for q2 in range(2):
-                    for u in range(2):
-                        nc.tensor.transpose(xt[:, q2, u, :], x_words[:, 2 * x2 + q2, :, u], ident_f32[:])
-                xt_view = xt[:].rearrange("k q u (m s) -> k m s q u", s=2)
-                if x2 == 0:
-                    nc.vector.tensor_copy(out=gx_words[:, x2], in_=xt_view)
-                else:
-                    nc.scalar.copy(out=gx_words[:, x2], in_=xt_view)
+        def turn_x(x2):
+            xt = psum.tile([P, 2, 2, P], F32, name="turn_%d" % x2)
+            for q2 in range(2):
+                for u in range(2):
+                    nc.tensor.transpose(xt[:, q2, u, :], x_words[:, 2 * x2 + q2, :, u], ident_f32[:])
+            xt_view = xt[:].rearrange("k q u (m s) -> k m s q u", s=2)
+            if x2 == 0:
+                nc.vector.tensor_copy(out=gx_words[:, x2], in_=xt_view)
+            else:
+                nc.scalar.copy(out=gx_words[:, x2], in_=xt_view)
 
         def quantise_x():
             nc.vector.quantize_mx(out=x_codes[:].bitcast(FP8X4), scales=x_scales[:], in_=grouped_x[:])
@@ -131,12 +132,12 @@ def tile_butterflylayer2d_pb_s_kernel(tc, x_leaf, f_first, b_first, f_second, b_
         b2_rep = keep.tile([P, CH], F32)
 
         def bias_1():
-            b1_ps = psum.tile([P, P], BF16)
+            b1_ps = psum.tile([P, P], BF16, name="b_ps")
             nc.tensor.transpose(b1_ps[:], b_rows[:], ident_bf16[:])
             nc.scalar.copy(out=b1_t[:], in_=b1_ps[:, 0:NODES])
 
         def bias_2():
-            b2_ps = psum.tile([P, CH], F32)
+            b2_ps = psum.tile([P, CH], F32, name="b_ps")
             nc.tensor.matmul(
                 b2_ps[:], lhsT=spread[:].rearrange("p n r -> p (n r)"), rhs=b_rows[:], start=True, stop=True
             )
@@ -151,7 +152,7 @@ def tile_butterflylayer2d_pb_s_kernel(tc, x_leaf, f_first, b_first, f_second, b_
                 node = first + n
                 c = node // WINDOW
                 if node % WINDOW == 0:
-                    h_ps[c] = psum.tile([P, WINDOW, WINDOW * ROWS1], F32, name="h_ps_%d" % (c % 2))
+                    h_ps[c] = psum.tile([P, WINDOW, WINDOW * ROWS1], F32, name="h_ps_%d" % c)
                 x_cols = slice(c * WINDOW * ROWS1, (c + 1) * WINDOW * ROWS1)
                 o_cols = slice(n * CH, (n + 1) * CH)
                 nc.tensor.matmul_mx(
@@ -182,6 +183,9 @@ def tile_butterflylayer2d_pb_s_kernel(tc, x_leaf, f_first, b_first, f_second, b_
             turned = psum.tile([P, PACK, CH], BF16, name="turn_0")
             for place in range(PACK):
                 nc.tensor.transpose(turned[:, place, :], h_by_channel[:, :, place], ident_bf16[:])
+            return turned
+
+        def keep_h_by_pixel(turned):
             nc.vector.tensor_copy(out=h_by_pixel[:], in_=turned[:].rearrange("m t o -> m (t o)"))
 
         def turn_h_to_k():
@@ -223,49 +227,55 @@ def tile_butterflylayer2d_pb_s_kernel(tc, x_leaf, f_first, b_first, f_second, b_
                     stop=(node == NODES - 1),
                 )
 
-        n1 = len(UNITS_1)
         copy(0)
         copy(1)
         quantise(0)
         copy(2)
         quantise(1)
-        turn_x()
-        bias_1()
         copy(3)
         quantise(2)
+        quantise(3)
+        turn_x(0)
+        turn_x(1)
+        bias_1()
+        bias_2()
+        copy(4)
         quantise_x()
-        for u in range(3):
+        for u in range(4):
             multiply_1(u)
-        for u in range(4, len(UNITS)):
-            copy(u)
-            if u == 4:
-                finish_1(0)
-            elif u == 5:
-                finish_1(1)
-                finish_1(2)
-            elif u == 6:
-                finish_1(3)
-                finish_1(4)
-            elif u - 2 < n1:
-                finish_1(u - 2)
-            quantise(u - 1)
-            if u - 1 < n1:
-                multiply_1(u - 1)
-            if u == n1 + 2:
-                turn_h_to_pixels()
-                bias_2()
-            if u == n1 + 3:
-                turn_h_to_k()
-            if u == n1 + 4:
-                quantise_h()
-            if u == n1 + 5:
-                spread_h()
-                for v in range(n1, u):
-                    multiply_2(v)
-            if u > n1 + 5:
-                multiply_2(u - 1)
-        quantise(len(UNITS) - 1)
-        multiply_2(len(UNITS) - 1)
+        copy(5)
+        quantise(4)
+        multiply_1(4)
+        for u in range(4):
+            finish_1(u)
+        quantise(5)
+        multiply_1(5)
+        finish_1(4)
+        finish_1(5)
+        turned = turn_h_to_pixels()
+        copy(6)
+        copy(7)
+        copy_vector(8)
+        keep_h_by_pixel(turned)
+        quantise(6)
+        turn_h_to_k()
+        copy_scalar(8)
+        quantise(7)
+        quantise_h()
+        copy(9)
+        spread_h()
+        multiply_2(6)
+        multiply_2(7)
+        quantise(8)
+        multiply_2(8)
+        quantise(9)
+        multiply_2(9)
+        copy(10)
+        copy(11)
+        quantise(10)
+        multiply_2(10)
+        quantise(11)
+        multiply_2(11)
 
         biased = keep.tile([P, CH], F32)
         nc.vector.tensor_tensor(out=biased[:], in0=out_ps[:], in1=b2_rep[:], op=ADD)

@@ -31,8 +31,8 @@ VECTOR_COLS = 72
 
 def regroup(copy, raw, grouped, o0, o1):
     copy(
-        out=grouped[:, :, o0:o1].rearrange("p n (c i) t -> p n c t i", i=4),
-        in_=raw[:, :, :, o0:o1].rearrange("p n t (c i) -> p n c t i", i=4),
+        out=grouped[:, :, o0:o1].rearrange("p n (c i) t -> p n c t i", i=8),
+        in_=raw[:, :, :, o0:o1].rearrange("p n t (c i) -> p n c t i", i=8),
     )
 
 
@@ -92,10 +92,10 @@ def tile_butterflylayer2d_pb_s_kernel(tc, x_leaf, f_first, b_first, f_second, b_
             w_scales.append(keep.tile([P, count * CH], U8, name="w_scales_%d" % u, align_bytes=64))
 
         def copy_vector(u):
-            regroup(nc.vector.tensor_copy, raw[u], grouped[u], 0, VECTOR_COLS)
+            regroup(nc.vector.tensor_copy, raw[u], grouped[u], 0, VECTOR_COLS if UNITS[u][2] > 1 else CH // 2)
 
         def copy_scalar(u):
-            regroup(nc.scalar.copy, raw[u], grouped[u], VECTOR_COLS, CH)
+            regroup(nc.scalar.copy, raw[u], grouped[u], VECTOR_COLS if UNITS[u][2] > 1 else CH // 2, CH)
 
         def copy(u):
             copy_vector(u)

@@ -23,7 +23,7 @@ DIAG = CH + ROWS2
 
 FLOPS = 2 * NODES * (ROWS1 + ROWS2) * (PACK * CH) * CH
 
-UNITS_1 = [(1, 0, 2), (1, 2, 2), (1, 4, 2), (1, 6, 2), (1, 8, 4), (1, 12, 4)]
+UNITS_1 = [(1, 0, 4), (1, 4, 4), (1, 8, 4), (1, 12, 4)]
 UNITS_2 = [(2, 0, 4), (2, 4, 4), (2, 8, 4), (2, 12, 2), (2, 14, 1), (2, 15, 1)]
 UNITS = UNITS_1 + UNITS_2
 VECTOR_COLS = 72
@@ -61,13 +61,12 @@ def tile_butterflylayer2d_pb_s_kernel(tc, x_leaf, f_first, b_first, f_second, b_
 
         b_rows = keep.tile([P, CH], BF16)
         nc.vector.memset(b_rows[:], 0.0)
-        for u in range(4):
-            load(u)
+        load(0)
         for x in range(4):
             nc.sync.dma_start(out=x_dst[:, x], in_=x_rows[x])
         nc.sync.dma_start(out=b_rows[0:NODES, :], in_=b_first.rearrange("a b o -> (a b) o"))
         nc.sync.dma_start(out=b_rows[NODES : 2 * NODES, :], in_=b_second.rearrange("a b o -> (a b) o"))
-        for u in range(4, len(UNITS)):
+        for u in range(1, len(UNITS)):
             load(u)
 
         ident_f32 = keep.tile([P, P], F32)
@@ -228,54 +227,46 @@ def tile_butterflylayer2d_pb_s_kernel(tc, x_leaf, f_first, b_first, f_second, b_
                 )
 
         copy(0)
-        copy(1)
         quantise(0)
-        copy(2)
-        quantise(1)
-        copy(3)
-        quantise(2)
-        quantise(3)
         turn_x(0)
         turn_x(1)
         bias_1()
-        bias_2()
-        copy(4)
+        copy(1)
         quantise_x()
-        for u in range(4):
-            multiply_1(u)
-        copy(5)
+        multiply_1(0)
+        copy(2)
+        quantise(1)
+        multiply_1(1)
+        finish_1(0)
+        copy(3)
+        quantise(2)
+        multiply_1(2)
+        finish_1(1)
+        quantise(3)
+        multiply_1(3)
+        copy(4)
+        finish_1(2)
+        finish_1(3)
         quantise(4)
-        multiply_1(4)
-        for u in range(4):
-            finish_1(u)
-        quantise(5)
-        multiply_1(5)
-        finish_1(4)
-        finish_1(5)
         turned = turn_h_to_pixels()
-        copy(6)
-        copy(7)
-        copy_vector(8)
+        copy(5)
         keep_h_by_pixel(turned)
-        quantise(6)
         turn_h_to_k()
-        copy_scalar(8)
-        quantise(7)
+        copy(6)
+        quantise(5)
         quantise_h()
-        copy(9)
         spread_h()
+        bias_2()
+        multiply_2(4)
+        multiply_2(5)
+        copy(7)
+        quantise(6)
         multiply_2(6)
-        multiply_2(7)
-        quantise(8)
-        multiply_2(8)
-        quantise(9)
-        multiply_2(9)
-        copy(10)
-        copy(11)
-        quantise(10)
-        multiply_2(10)
-        quantise(11)
-        multiply_2(11)
+        copy(8)
+        copy(9)
+        for u in range(7, 10):
+            quantise(u)
+            multiply_2(u)
 
         biased = keep.tile([P, CH], F32)
         nc.vector.tensor_tensor(out=biased[:], in0=out_ps[:], in1=b2_rep[:], op=ADD)

@@ -175,6 +175,19 @@ def tile_butterflylayer2d_pb_s_kernel(tc, x_leaf, f_first, b_first, f_second, b_
                     bias=b1_t[:, node : node + 1],
                 )
 
+        def keep_clock_up(passes):
+            unread = psum.tile([P, 4 * CH], F32, name="h_ps_0")
+            for i in range(passes):
+                nc.tensor.matmul_mx(
+                    out=unread[:],
+                    lhsT=w_codes[3][:, 0:CH].bitcast(FP8X4),
+                    lhsT_scale=w_scales[3][:, 0:CH],
+                    rhs=w_codes[3][:].bitcast(FP8X4),
+                    rhs_scale=w_scales[3][:],
+                    start=True,
+                    stop=True,
+                )
+
         h_by_pixel = keep.tile([P, PACK * CH], BF16)
         grouped_h = keep.tile([P, NODES * ROWS2 * PACK], BF16, align_bytes=64)
 
@@ -182,6 +195,7 @@ def tile_butterflylayer2d_pb_s_kernel(tc, x_leaf, f_first, b_first, f_second, b_
             turned = psum.tile([P, PACK, CH], BF16, name="turn_0")
             for place in range(PACK):
                 nc.tensor.transpose(turned[:, place, :], h_by_channel[:, :, place], ident_bf16[:])
+            keep_clock_up(2)
             return turned
 
         def keep_h_by_pixel(turned):
@@ -192,6 +206,7 @@ def tile_butterflylayer2d_pb_s_kernel(tc, x_leaf, f_first, b_first, f_second, b_
             turned = psum.tile([P, 2, P], F32, name="turn_1")
             for u in range(2):
                 nc.tensor.transpose(turned[:, u, :], words[:, :, u], ident_f32[:])
+            keep_clock_up(3)
             nc.scalar.copy(
                 out=grouped_h[:].bitcast(F32).rearrange("k (m u) -> k m u", u=2),
                 in_=turned[:].rearrange("k u m -> k m u"),

@@ -175,15 +175,15 @@ def tile_butterflylayer2d_pb_s_kernel(tc, x_leaf, f_first, b_first, f_second, b_
                     bias=b1_t[:, node : node + 1],
                 )
 
-        def keep_clock_up(passes):
-            unread = psum.tile([P, 4 * CH], F32, name="h_ps_0")
+        def keep_clock_up(u, passes):
+            unread = psum.tile([P, WINDOW * CH], F32, name="out_ps")
             for i in range(passes):
                 nc.tensor.matmul_mx(
                     out=unread[:],
-                    lhsT=w_codes[3][:, 0:CH].bitcast(FP8X4),
-                    lhsT_scale=w_scales[3][:, 0:CH],
-                    rhs=w_codes[3][:].bitcast(FP8X4),
-                    rhs_scale=w_scales[3][:],
+                    lhsT=w_codes[u][:, 0:CH].bitcast(FP8X4),
+                    lhsT_scale=w_scales[u][:, 0:CH],
+                    rhs=w_codes[u][:].bitcast(FP8X4),
+                    rhs_scale=w_scales[u][:],
                     start=True,
                     stop=True,
                 )
@@ -192,10 +192,10 @@ def tile_butterflylayer2d_pb_s_kernel(tc, x_leaf, f_first, b_first, f_second, b_
         grouped_h = keep.tile([P, NODES * ROWS2 * PACK], BF16, align_bytes=64)
 
         def turn_h_to_pixels():
+            keep_clock_up(3, 2)
             turned = psum.tile([P, PACK, CH], BF16, name="turn_0")
             for place in range(PACK):
                 nc.tensor.transpose(turned[:, place, :], h_by_channel[:, :, place], ident_bf16[:])
-            keep_clock_up(2)
             return turned
 
         def keep_h_by_pixel(turned):
@@ -206,7 +206,7 @@ def tile_butterflylayer2d_pb_s_kernel(tc, x_leaf, f_first, b_first, f_second, b_
             turned = psum.tile([P, 2, P], F32, name="turn_1")
             for u in range(2):
                 nc.tensor.transpose(turned[:, u, :], words[:, :, u], ident_f32[:])
-            keep_clock_up(3)
+            keep_clock_up(3, 3)
             nc.scalar.copy(
                 out=grouped_h[:].bitcast(F32).rearrange("k (m u) -> k m u", u=2),
                 in_=turned[:].rearrange("k u m -> k m u"),
@@ -224,9 +224,7 @@ def tile_butterflylayer2d_pb_s_kernel(tc, x_leaf, f_first, b_first, f_second, b_
                 in_=h_codes[:].bitcast(I32).rearrange("k (i s) -> k i s", s=ROWS2),
             )
 
-        out_ps = psum.tile([P, CH], F32)
-
-        def multiply_2(u):
+        def multiply_2(u, out_ps):
             level, first, count = UNITS[u]
             for n in range(count):
                 node = first + n
@@ -248,14 +246,18 @@ def tile_butterflylayer2d_pb_s_kernel(tc, x_leaf, f_first, b_first, f_second, b_
         bias_1()
         copy(1)
         quantise_x()
+        keep_clock_up(0, 4)
         multiply_1(0)
+        keep_clock_up(0, 1)
         copy(2)
         quantise(1)
         multiply_1(1)
+        keep_clock_up(0, 1)
         finish_1(0)
         copy(3)
         quantise(2)
         multiply_1(2)
+        keep_clock_up(0, 1)
         finish_1(1)
         quantise(3)
         multiply_1(3)
@@ -272,16 +274,17 @@ def tile_butterflylayer2d_pb_s_kernel(tc, x_leaf, f_first, b_first, f_second, b_
         quantise_h()
         spread_h()
         bias_2()
-        multiply_2(4)
-        multiply_2(5)
+        out_ps = psum.tile([P, CH], F32)
+        multiply_2(4, out_ps)
+        multiply_2(5, out_ps)
         copy(7)
         quantise(6)
-        multiply_2(6)
+        multiply_2(6, out_ps)
         copy(8)
         copy(9)
         for u in range(7, 10):
             quantise(u)
-            multiply_2(u)
+            multiply_2(u, out_ps)
 
         biased = keep.tile([P, CH], F32)
         nc.vector.tensor_tensor(out=biased[:], in0=out_ps[:], in1=b2_rep[:], op=ADD)

@@ -24,9 +24,9 @@ DIAG = CH + ROWS2
 FLOPS = 2 * NODES * (ROWS1 + ROWS2) * (PACK * CH) * CH
 
 UNITS_1 = [(1, 0, 4), (1, 4, 4), (1, 8, 4), (1, 12, 4)]
-UNITS_2 = [(2, 0, 4), (2, 4, 4), (2, 8, 4), (2, 12, 2), (2, 14, 1), (2, 15, 1)]
+UNITS_2 = [(2, 0, 4), (2, 4, 4), (2, 8, 4), (2, 12, 2), (2, 14, 2)]
 UNITS = UNITS_1 + UNITS_2
-VECTOR_COLS = 72
+VECTOR_COLS = {4: 72, 2: 56}
 
 
 def regroup(copy, raw, grouped, o0, o1):
@@ -62,10 +62,10 @@ def tile_butterflylayer2d_pb_s_kernel(tc, x_leaf, f_first, b_first, f_second, b_
         b_rows = keep.tile([P, CH], BF16)
         nc.vector.memset(b_rows[:], 0.0)
         load(0)
-        for x in range(4):
-            nc.sync.dma_start(out=x_dst[:, x], in_=x_rows[x])
         nc.sync.dma_start(out=b_rows[0:NODES, :], in_=b_first.rearrange("a b o -> (a b) o"))
         nc.sync.dma_start(out=b_rows[NODES : 2 * NODES, :], in_=b_second.rearrange("a b o -> (a b) o"))
+        for x in range(4):
+            nc.sync.dma_start(out=x_dst[:, x], in_=x_rows[x])
         for u in range(1, len(UNITS)):
             load(u)
 
@@ -91,10 +91,10 @@ def tile_butterflylayer2d_pb_s_kernel(tc, x_leaf, f_first, b_first, f_second, b_
             w_scales.append(keep.tile([P, count * CH], U8, name="w_scales_%d" % u, align_bytes=64))
 
         def copy_vector(u):
-            regroup(nc.vector.tensor_copy, raw[u], grouped[u], 0, VECTOR_COLS if UNITS[u][2] > 1 else CH // 2)
+            regroup(nc.vector.tensor_copy, raw[u], grouped[u], 0, VECTOR_COLS[UNITS[u][2]])
 
         def copy_scalar(u):
-            regroup(nc.scalar.copy, raw[u], grouped[u], VECTOR_COLS if UNITS[u][2] > 1 else CH // 2, CH)
+            regroup(nc.scalar.copy, raw[u], grouped[u], VECTOR_COLS[UNITS[u][2]], CH)
 
         def copy(u):
             copy_vector(u)
@@ -136,7 +136,7 @@ def tile_butterflylayer2d_pb_s_kernel(tc, x_leaf, f_first, b_first, f_second, b_
             nc.scalar.copy(out=b1_t[:], in_=b1_ps[:, 0:NODES])
 
         def bias_2():
-            b2_ps = psum.tile([P, CH], F32, name="b_ps")
+            b2_ps = psum.tile([P, CH], F32, name="h_ps_3")
             nc.tensor.matmul(
                 b2_ps[:], lhsT=spread[:].rearrange("p n r -> p (n r)"), rhs=b_rows[:], start=True, stop=True
             )
@@ -240,49 +240,46 @@ def tile_butterflylayer2d_pb_s_kernel(tc, x_leaf, f_first, b_first, f_second, b_
                 )
 
         copy(0)
-        quantise(0)
-        turn_x(0)
-        turn_x(1)
         bias_1()
-        copy(1)
+        bias_2()
+        turn_x(0)
+        quantise(0)
+        turn_x(1)
         quantise_x()
-        keep_clock_up(0, 4)
-        multiply_1(0)
         keep_clock_up(0, 1)
+        multiply_1(0)
+        keep_clock_up(0, 3)
+        copy(1)
         copy(2)
         quantise(1)
         multiply_1(1)
-        keep_clock_up(0, 1)
+        keep_clock_up(0, 2)
         finish_1(0)
         copy(3)
         quantise(2)
         multiply_1(2)
-        keep_clock_up(0, 1)
-        finish_1(1)
         quantise(3)
         multiply_1(3)
         copy(4)
-        finish_1(2)
-        finish_1(3)
-        quantise(4)
+        for u in range(1, 4):
+            finish_1(u)
         turned = turn_h_to_pixels()
         copy(5)
+        quantise(4)
         keep_h_by_pixel(turned)
         turn_h_to_k()
         copy(6)
-        quantise(5)
         quantise_h()
+        copy(7)
         spread_h()
-        bias_2()
         out_ps = psum.tile([P, CH], F32)
         multiply_2(4, out_ps)
+        quantise(5)
         multiply_2(5, out_ps)
-        copy(7)
         quantise(6)
         multiply_2(6, out_ps)
         copy(8)
-        copy(9)
-        for u in range(7, 10):
+        for u in range(7, 9):
             quantise(u)
             multiply_2(u, out_ps)
 

@@ -23,7 +23,7 @@ DIAG = CH + ROWS2
 
 FLOPS = 2 * NODES * (ROWS1 + ROWS2) * (PACK * CH) * CH
 
-UNITS_1 = [(1, 0, 4), (1, 4, 4), (1, 8, 4), (1, 12, 4)]
+UNITS_1 = [(1, 0, 2), (1, 2, 2), (1, 4, 2), (1, 6, 2), (1, 8, 4), (1, 12, 4)]
 UNITS_2 = [(2, 0, 4), (2, 4, 4), (2, 8, 4), (2, 12, 2), (2, 14, 2)]
 UNITS = UNITS_1 + UNITS_2
 VECTOR_COLS = {4: 72, 2: 56}
@@ -61,12 +61,14 @@ def tile_butterflylayer2d_pb_s_kernel(tc, x_leaf, f_first, b_first, f_second, b_
 
         b_rows = keep.tile([P, CH], BF16)
         nc.vector.memset(b_rows[:], 0.0)
-        load(0)
-        nc.sync.dma_start(out=b_rows[0:NODES, :], in_=b_first.rearrange("a b o -> (a b) o"))
-        nc.sync.dma_start(out=b_rows[NODES : 2 * NODES, :], in_=b_second.rearrange("a b o -> (a b) o"))
         for x in range(4):
             nc.sync.dma_start(out=x_dst[:, x], in_=x_rows[x])
-        for u in range(1, len(UNITS)):
+            if x == 0:
+                nc.scalar.dma_start(out=b_rows[0:NODES, :], in_=b_first.rearrange("a b o -> (a b) o"))
+                nc.scalar.dma_start(out=b_rows[NODES : 2 * NODES, :], in_=b_second.rearrange("a b o -> (a b) o"))
+        for u in range(4):
+            load(u)
+        for u in range(4, len(UNITS)):
             load(u)
 
         ident_f32 = keep.tile([P, P], F32)
@@ -119,10 +121,7 @@ def tile_butterflylayer2d_pb_s_kernel(tc, x_leaf, f_first, b_first, f_second, b_
                 for u in range(2):
                     nc.tensor.transpose(xt[:, q2, u, :], x_words[:, 2 * x2 + q2, :, u], ident_f32[:])
             xt_view = xt[:].rearrange("k q u (m s) -> k m s q u", s=2)
-            if x2 == 0:
-                nc.vector.tensor_copy(out=gx_words[:, x2], in_=xt_view)
-            else:
-                nc.scalar.copy(out=gx_words[:, x2], in_=xt_view)
+            nc.vector.tensor_copy(out=gx_words[:, x2], in_=xt_view)
 
         def quantise_x():
             nc.vector.quantize_mx(out=x_codes[:].bitcast(FP8X4), scales=x_scales[:], in_=grouped_x[:])
@@ -176,10 +175,11 @@ def tile_butterflylayer2d_pb_s_kernel(tc, x_leaf, f_first, b_first, f_second, b_
                 )
 
         def keep_clock_up(u, passes):
+            level, first, count = UNITS[u]
             unread = psum.tile([P, WINDOW * CH], F32, name="out_ps")
             for i in range(passes):
                 nc.tensor.matmul_mx(
-                    out=unread[:],
+                    out=unread[:, 0 : count * CH],
                     lhsT=w_codes[u][:, 0:CH].bitcast(FP8X4),
                     lhsT_scale=w_scales[u][:, 0:CH],
                     rhs=w_codes[u][:].bitcast(FP8X4),
@@ -192,7 +192,7 @@ def tile_butterflylayer2d_pb_s_kernel(tc, x_leaf, f_first, b_first, f_second, b_
         grouped_h = keep.tile([P, NODES * ROWS2 * PACK], BF16, align_bytes=64)
 
         def turn_h_to_pixels():
-            keep_clock_up(3, 2)
+            keep_clock_up(4, 2)
             turned = psum.tile([P, PACK, CH], BF16, name="turn_0")
             for place in range(PACK):
                 nc.tensor.transpose(turned[:, place, :], h_by_channel[:, :, place], ident_bf16[:])
@@ -201,12 +201,15 @@ def tile_butterflylayer2d_pb_s_kernel(tc, x_leaf, f_first, b_first, f_second, b_
         def keep_h_by_pixel(turned):
             nc.vector.tensor_copy(out=h_by_pixel[:], in_=turned[:].rearrange("m t o -> m (t o)"))
 
-        def turn_h_to_k():
+        def turn_h_to_k_t():
             words = h_by_pixel[:].bitcast(F32).rearrange("m (k u) -> m k u", u=2)
             turned = psum.tile([P, 2, P], F32, name="turn_1")
             for u in range(2):
                 nc.tensor.transpose(turned[:, u, :], words[:, :, u], ident_f32[:])
-            keep_clock_up(3, 3)
+            keep_clock_up(4, 3)
+            return turned
+
+        def turn_h_to_k_s(turned):
             nc.scalar.copy(
                 out=grouped_h[:].bitcast(F32).rearrange("k (m u) -> k m u", u=2),
                 in_=turned[:].rearrange("k u m -> k m u"),
@@ -239,47 +242,55 @@ def tile_butterflylayer2d_pb_s_kernel(tc, x_leaf, f_first, b_first, f_second, b_
                     stop=(node == NODES - 1),
                 )
 
+        turn_x(0)
+        turn_x(1)
         copy(0)
+        quantise_x()
         bias_1()
         bias_2()
-        turn_x(0)
-        quantise(0)
-        turn_x(1)
-        quantise_x()
-        keep_clock_up(0, 1)
-        multiply_1(0)
-        keep_clock_up(0, 3)
         copy(1)
+        quantise(0)
+        keep_clock_up(0, 3)
+        multiply_1(0)
         copy(2)
         quantise(1)
         multiply_1(1)
-        keep_clock_up(0, 2)
-        finish_1(0)
+        keep_clock_up(1, 3)
         copy(3)
         quantise(2)
         multiply_1(2)
+        keep_clock_up(1, 3)
+        copy(4)
         quantise(3)
         multiply_1(3)
-        copy(4)
-        for u in range(1, 4):
-            finish_1(u)
-        turned = turn_h_to_pixels()
         copy(5)
+        for u in range(3):
+            finish_1(u)
         quantise(4)
-        keep_h_by_pixel(turned)
-        turn_h_to_k()
+        multiply_1(4)
+        quantise(5)
+        multiply_1(5)
         copy(6)
-        quantise_h()
+        for u in range(3, 6):
+            finish_1(u)
         copy(7)
+        turned = turn_h_to_pixels()
+        quantise(6)
+        copy(8)
+        keep_h_by_pixel(turned)
+        turned_k = turn_h_to_k_t()
+        turn_h_to_k_s(turned_k)
+        copy(9)
+        quantise(7)
+        quantise_h()
+        copy(10)
         spread_h()
         out_ps = psum.tile([P, CH], F32)
-        multiply_2(4, out_ps)
-        quantise(5)
-        multiply_2(5, out_ps)
-        quantise(6)
         multiply_2(6, out_ps)
-        copy(8)
-        for u in range(7, 9):
+        multiply_2(7, out_ps)
+        quantise(8)
+        multiply_2(8, out_ps)
+        for u in range(9, 11):
             quantise(u)
             multiply_2(u, out_ps)
 

@@ -174,16 +174,15 @@ def tile_butterflylayer2d_pb_s_kernel(tc, x_leaf, f_first, b_first, f_second, b_
                     bias=b1_t[:, node : node + 1],
                 )
 
-        def keep_clock_up(u, passes):
-            level, first, count = UNITS[u]
-            unread = psum.tile([P, WINDOW * CH], F32, name="out_ps")
+        def keep_clock_up(passes):
+            unread = psum.tile([P, NODES * ROWS1], F32, name="out_ps")
             for i in range(passes):
                 nc.tensor.matmul_mx(
-                    out=unread[:, 0 : count * CH],
-                    lhsT=w_codes[u][:, 0:CH].bitcast(FP8X4),
-                    lhsT_scale=w_scales[u][:, 0:CH],
-                    rhs=w_codes[u][:].bitcast(FP8X4),
-                    rhs_scale=w_scales[u][:],
+                    out=unread[:],
+                    lhsT=w_codes[0][:, 0:CH].bitcast(FP8X4),
+                    lhsT_scale=w_scales[0][:, 0:CH],
+                    rhs=x_codes[:].bitcast(FP8X4),
+                    rhs_scale=x_scales[:],
                     start=True,
                     stop=True,
                 )
@@ -192,7 +191,7 @@ def tile_butterflylayer2d_pb_s_kernel(tc, x_leaf, f_first, b_first, f_second, b_
         grouped_h = keep.tile([P, NODES * ROWS2 * PACK], BF16, align_bytes=64)
 
         def turn_h_to_pixels():
-            keep_clock_up(4, 2)
+            keep_clock_up(2)
             turned = psum.tile([P, PACK, CH], BF16, name="turn_0")
             for place in range(PACK):
                 nc.tensor.transpose(turned[:, place, :], h_by_channel[:, :, place], ident_bf16[:])
@@ -206,7 +205,7 @@ def tile_butterflylayer2d_pb_s_kernel(tc, x_leaf, f_first, b_first, f_second, b_
             turned = psum.tile([P, 2, P], F32, name="turn_1")
             for u in range(2):
                 nc.tensor.transpose(turned[:, u, :], words[:, :, u], ident_f32[:])
-            keep_clock_up(4, 3)
+            keep_clock_up(5)
             return turned
 
         def turn_h_to_k_s(turned):
@@ -250,24 +249,27 @@ def tile_butterflylayer2d_pb_s_kernel(tc, x_leaf, f_first, b_first, f_second, b_
         bias_2()
         copy(1)
         quantise(0)
-        keep_clock_up(0, 3)
+        keep_clock_up(2)
         multiply_1(0)
+        keep_clock_up(2)
         copy(2)
         quantise(1)
         multiply_1(1)
-        keep_clock_up(1, 3)
+        keep_clock_up(1)
         copy(3)
         quantise(2)
         multiply_1(2)
-        keep_clock_up(1, 3)
+        keep_clock_up(1)
         copy(4)
         quantise(3)
         multiply_1(3)
+        keep_clock_up(1)
         copy(5)
         for u in range(3):
             finish_1(u)
         quantise(4)
         multiply_1(4)
+        keep_clock_up(1)
         quantise(5)
         multiply_1(5)
         copy(6)
@@ -275,6 +277,7 @@ def tile_butterflylayer2d_pb_s_kernel(tc, x_leaf, f_first, b_first, f_second, b_
             finish_1(u)
         copy(7)
         turned = turn_h_to_pixels()
+        keep_clock_up(2)
         quantise(6)
         copy(8)
         keep_h_by_pixel(turned)

@@ -29,10 +29,10 @@ UNITS = UNITS_1 + UNITS_2
 VECTOR_COLS = {4: 72, 2: 56}
 
 
-def regroup(copy, raw, grouped, o0, o1):
+def regroup(copy, raw, grouped, o0, o1, run):
     copy(
-        out=grouped[:, :, o0:o1].rearrange("p n (c i) t -> p n c t i", i=8),
-        in_=raw[:, :, :, o0:o1].rearrange("p n t (c i) -> p n c t i", i=8),
+        out=grouped[:, :, o0:o1].rearrange("p n (c i) t -> p n c t i", i=run),
+        in_=raw[:, :, :, o0:o1].rearrange("p n t (c i) -> p n c t i", i=run),
     )
 
 
@@ -93,10 +93,10 @@ def tile_butterflylayer2d_pb_s_kernel(tc, x_leaf, f_first, b_first, f_second, b_
             w_scales.append(keep.tile([P, count * CH], U8, name="w_scales_%d" % u, align_bytes=64))
 
         def copy_vector(u):
-            regroup(nc.vector.tensor_copy, raw[u], grouped[u], 0, VECTOR_COLS[UNITS[u][2]])
+            regroup(nc.vector.tensor_copy, raw[u], grouped[u], 0, VECTOR_COLS[UNITS[u][2]], 4)
 
         def copy_scalar(u):
-            regroup(nc.scalar.copy, raw[u], grouped[u], VECTOR_COLS[UNITS[u][2]], CH)
+            regroup(nc.scalar.copy, raw[u], grouped[u], VECTOR_COLS[UNITS[u][2]], CH, 8)
 
         def copy(u):
             copy_vector(u)
@@ -205,7 +205,7 @@ def tile_butterflylayer2d_pb_s_kernel(tc, x_leaf, f_first, b_first, f_second, b_
             turned = psum.tile([P, 2, P], F32, name="turn_1")
             for u in range(2):
                 nc.tensor.transpose(turned[:, u, :], words[:, :, u], ident_f32[:])
-            keep_clock_up(5)
+            keep_clock_up(3)
             return turned
 
         def turn_h_to_k_s(turned):

@@ -23,16 +23,13 @@ DIAG = CH + ROWS2
 
 FLOPS = 2 * NODES * (ROWS1 + ROWS2) * (PACK * CH) * CH
 
-UNITS_1 = [(1, 0, 2), (1, 2, 2), (1, 4, 2), (1, 6, 2), (1, 8, 4), (1, 12, 4)]
-UNITS_2 = [(2, 0, 4), (2, 4, 4), (2, 8, 4), (2, 12, 2), (2, 14, 2)]
-UNITS = UNITS_1 + UNITS_2
-VECTOR_COLS = {4: 72, 2: 56}
+UNITS = [(level, node, 2, "sv"[node // 2 % 2]) for level in (1, 2) for node in range(0, NODES, 2)]
 
 
-def regroup(copy, raw, grouped, o0, o1, run):
+def regroup(copy, raw, grouped):
     copy(
-        out=grouped[:, :, o0:o1].rearrange("p n (c i) t -> p n c t i", i=run),
-        in_=raw[:, :, :, o0:o1].rearrange("p n t (c i) -> p n c t i", i=run),
+        out=grouped[:].rearrange("p n (c i) t -> p n c t i", i=4),
+        in_=raw[:].rearrange("p n t (c i) -> p n c t i", i=4),
     )
 
 
@@ -48,11 +45,11 @@ def tile_butterflylayer2d_pb_s_kernel(tc, x_leaf, f_first, b_first, f_second, b_
             for level, f in ((1, f_first), (2, f_second))
         }
         raw = []
-        for u, (level, node, count) in enumerate(UNITS):
+        for u, (level, node, count, engine) in enumerate(UNITS):
             raw.append(keep.tile([P, count, PACK, CH], BF16, name="raw_%d" % u))
 
         def load(u):
-            level, node, count = UNITS[u]
+            level, node, count, engine = UNITS[u]
             nc.sync.dma_start(out=raw[u][:], in_=w_rows[level][:, node : node + count])
 
         x_sb = keep.tile([P, 4 * PACK * CH], BF16)
@@ -63,12 +60,10 @@ def tile_butterflylayer2d_pb_s_kernel(tc, x_leaf, f_first, b_first, f_second, b_
         nc.vector.memset(b_rows[:], 0.0)
         for x in range(4):
             nc.sync.dma_start(out=x_dst[:, x], in_=x_rows[x])
-            if x == 0:
-                nc.scalar.dma_start(out=b_rows[0:NODES, :], in_=b_first.rearrange("a b o -> (a b) o"))
-                nc.scalar.dma_start(out=b_rows[NODES : 2 * NODES, :], in_=b_second.rearrange("a b o -> (a b) o"))
-        for u in range(4):
-            load(u)
-        for u in range(4, len(UNITS)):
+        load(0)
+        nc.sync.dma_start(out=b_rows[0:NODES, :], in_=b_first.rearrange("a b o -> (a b) o"))
+        nc.sync.dma_start(out=b_rows[NODES : 2 * NODES, :], in_=b_second.rearrange("a b o -> (a b) o"))
+        for u in range(1, len(UNITS)):
             load(u)
 
         ident_f32 = keep.tile([P, P], F32)
@@ -87,20 +82,13 @@ def tile_butterflylayer2d_pb_s_kernel(tc, x_leaf, f_first, b_first, f_second, b_
         grouped = []
         w_codes = []
         w_scales = []
-        for u, (level, node, count) in enumerate(UNITS):
+        for u, (level, node, count, engine) in enumerate(UNITS):
             grouped.append(keep.tile([P, count, CH, PACK], BF16, name="grouped_%d" % u, align_bytes=64))
             w_codes.append(keep.tile([P, count * CH], U32, name="w_codes_%d" % u, align_bytes=64))
             w_scales.append(keep.tile([P, count * CH], U8, name="w_scales_%d" % u, align_bytes=64))
 
-        def copy_vector(u):
-            regroup(nc.vector.tensor_copy, raw[u], grouped[u], 0, VECTOR_COLS[UNITS[u][2]], 4)
-
-        def copy_scalar(u):
-            regroup(nc.scalar.copy, raw[u], grouped[u], VECTOR_COLS[UNITS[u][2]], CH, 8)
-
         def copy(u):
-            copy_vector(u)
-            copy_scalar(u)
+            regroup(nc.scalar.copy if UNITS[u][3] == "s" else nc.vector.tensor_copy, raw[u], grouped[u])
 
         def quantise(u):
             nc.vector.quantize_mx(
@@ -145,11 +133,11 @@ def tile_butterflylayer2d_pb_s_kernel(tc, x_leaf, f_first, b_first, f_second, b_
         h_ps = {}
 
         def multiply_1(u):
-            level, first, count = UNITS[u]
+            level, first, count, engine = UNITS[u]
             for n in range(count):
                 node = first + n
                 c = node // WINDOW
-                if node % WINDOW == 0:
+                if c not in h_ps:
                     h_ps[c] = psum.tile([P, WINDOW, WINDOW * ROWS1], F32, name="h_ps_%d" % c)
                 x_cols = slice(c * WINDOW * ROWS1, (c + 1) * WINDOW * ROWS1)
                 o_cols = slice(n * CH, (n + 1) * CH)
@@ -164,7 +152,7 @@ def tile_butterflylayer2d_pb_s_kernel(tc, x_leaf, f_first, b_first, f_second, b_
                 )
 
         def finish_1(u):
-            level, first, count = UNITS[u]
+            level, first, count, engine = UNITS[u]
             for node in range(first, first + count):
                 n = node % WINDOW
                 nc.scalar.activation(
@@ -179,8 +167,8 @@ def tile_butterflylayer2d_pb_s_kernel(tc, x_leaf, f_first, b_first, f_second, b_
             for i in range(passes):
                 nc.tensor.matmul_mx(
                     out=unread[:],
-                    lhsT=w_codes[0][:, 0:CH].bitcast(FP8X4),
-                    lhsT_scale=w_scales[0][:, 0:CH],
+                    lhsT=w_codes[1][:, 0:CH].bitcast(FP8X4),
+                    lhsT_scale=w_scales[1][:, 0:CH],
                     rhs=x_codes[:].bitcast(FP8X4),
                     rhs_scale=x_scales[:],
                     start=True,
@@ -226,8 +214,8 @@ def tile_butterflylayer2d_pb_s_kernel(tc, x_leaf, f_first, b_first, f_second, b_
                 in_=h_codes[:].bitcast(I32).rearrange("k (i s) -> k i s", s=ROWS2),
             )
 
-        def multiply_2(u, out_ps):
-            level, first, count = UNITS[u]
+        def multiply_2(u, out_ps, start=False, stop=False):
+            level, first, count, engine = UNITS[u]
             for n in range(count):
                 node = first + n
                 o_cols = slice(n * CH, (n + 1) * CH)
@@ -237,65 +225,65 @@ def tile_butterflylayer2d_pb_s_kernel(tc, x_leaf, f_first, b_first, f_second, b_
                     lhsT_scale=h_scales[:],
                     rhs=w_codes[u][:, o_cols].bitcast(FP8X4),
                     rhs_scale=w_scales[u][:, o_cols],
-                    start=(node == 0),
-                    stop=(node == NODES - 1),
+                    start=(start and n == 0),
+                    stop=(stop and n == count - 1),
                 )
 
         turn_x(0)
         turn_x(1)
         copy(0)
+        copy(1)
         quantise_x()
         bias_1()
         bias_2()
-        copy(1)
-        quantise(0)
-        keep_clock_up(2)
-        multiply_1(0)
-        keep_clock_up(2)
-        copy(2)
-        quantise(1)
-        multiply_1(1)
-        keep_clock_up(1)
-        copy(3)
-        quantise(2)
-        multiply_1(2)
-        keep_clock_up(1)
-        copy(4)
-        quantise(3)
-        multiply_1(3)
-        keep_clock_up(1)
-        copy(5)
-        for u in range(3):
+        for u in range(2, 8, 2):
+            copy(u)
+            copy(u + 1)
+            quantise(u - 1)
+            if u == 2:
+                keep_clock_up(2)
+            multiply_1(u - 1)
+            quantise(u - 2)
+            keep_clock_up(1)
+            multiply_1(u - 2)
+        copy(8)
+        for u in range(4):
             finish_1(u)
-        quantise(4)
-        multiply_1(4)
+        quantise(7)
+        multiply_1(7)
+        quantise(6)
         keep_clock_up(1)
-        quantise(5)
-        multiply_1(5)
-        copy(6)
-        for u in range(3, 6):
+        multiply_1(6)
+        copy(9)
+        for u in range(4, 8):
             finish_1(u)
-        copy(7)
+        copy(10)
+        copy(11)
         turned = turn_h_to_pixels()
         keep_clock_up(2)
-        quantise(6)
-        copy(8)
+        quantise(9)
+        quantise(8)
+        copy(12)
+        copy(13)
         keep_h_by_pixel(turned)
         turned_k = turn_h_to_k_t()
         turn_h_to_k_s(turned_k)
-        copy(9)
-        quantise(7)
+        quantise(11)
+        quantise(10)
+        copy(14)
+        copy(15)
         quantise_h()
-        copy(10)
+        quantise(13)
         spread_h()
+        quantise(12)
         out_ps = psum.tile([P, CH], F32)
-        multiply_2(6, out_ps)
-        multiply_2(7, out_ps)
-        quantise(8)
-        multiply_2(8, out_ps)
-        for u in range(9, 11):
-            quantise(u)
+        multiply_2(9, out_ps, start=True)
+        for u in (8, 11, 10, 13, 12):
             multiply_2(u, out_ps)
+        quantise(15)
+        multiply_2(15, out_ps)
+        quantise(14)
+        multiply_2(14, out_ps, stop=True)
 
         biased = keep.tile([P, CH], F32)
         nc.vector.tensor_tensor(out=biased[:], in0=out_ps[:], in1=b2_rep[:], op=ADD)

@@ -24,6 +24,7 @@ DIAG = CH + ROWS2
 FLOPS = 2 * NODES * (ROWS1 + ROWS2) * (PACK * CH) * CH
 
 UNITS = [(level, node, 2, "sv"[node // 2 % 2]) for level in (1, 2) for node in range(0, NODES, 2)]
+UNITS[-1:] = [(2, 14, 1, "v"), (2, 15, 1, "s")]
 
 
 def regroup(copy, raw, grouped):
@@ -99,17 +100,17 @@ def tile_butterflylayer2d_pb_s_kernel(tc, x_leaf, f_first, b_first, f_second, b_
 
         x_words = x_sb[:].bitcast(F32).rearrange("r (x k u) -> r x k u", x=4, u=2)
         grouped_x = keep.tile([P, NODES * ROWS1 * PACK], BF16, align_bytes=64)
-        gx_words = grouped_x[:].bitcast(F32).rearrange("k (m x s q u) -> k x m s q u", x=2, s=2, q=2, u=2)
+        gx_words = grouped_x[:].bitcast(F32).rearrange("k (m x q s u) -> k x q m s u", x=2, s=2, q=2, u=2)
         x_codes = keep.tile([P, NODES * ROWS1], U32, align_bytes=64)
         x_scales = keep.tile([P, NODES * ROWS1], U8, align_bytes=64)
 
-        def turn_x(x2):
-            xt = psum.tile([P, 2, 2, P], F32, name="turn_%d" % x2)
-            for q2 in range(2):
-                for u in range(2):
-                    nc.tensor.transpose(xt[:, q2, u, :], x_words[:, 2 * x2 + q2, :, u], ident_f32[:])
-            xt_view = xt[:].rearrange("k q u (m s) -> k m s q u", s=2)
-            nc.vector.tensor_copy(out=gx_words[:, x2], in_=xt_view)
+        def turn_x(x, bank):
+            xt = psum.tile([P, 2, P], F32, name=bank)
+            for u in range(2):
+                nc.tensor.transpose(xt[:, u, :], x_words[:, x, :, u], ident_f32[:])
+            nc.vector.tensor_copy(
+                out=gx_words[:, x // 2, x % 2], in_=xt[:].rearrange("k u (m s) -> k m s u", s=2)
+            )
 
         def quantise_x():
             nc.vector.quantize_mx(out=x_codes[:].bitcast(FP8X4), scales=x_scales[:], in_=grouped_x[:])
@@ -138,11 +139,12 @@ def tile_butterflylayer2d_pb_s_kernel(tc, x_leaf, f_first, b_first, f_second, b_
                 node = first + n
                 c = node // WINDOW
                 if c not in h_ps:
-                    h_ps[c] = psum.tile([P, WINDOW, WINDOW * ROWS1], F32, name="h_ps_%d" % c)
+                    h_ps[c] = psum.tile([P, WINDOW * WINDOW * ROWS1], F32, name="h_ps_%d" % c)
+                out_0 = (node % WINDOW) * (WINDOW - 1) * ROWS1
                 x_cols = slice(c * WINDOW * ROWS1, (c + 1) * WINDOW * ROWS1)
                 o_cols = slice(n * CH, (n + 1) * CH)
                 nc.tensor.matmul_mx(
-                    out=h_ps[c][:, node % WINDOW, :],
+                    out=h_ps[c][:, out_0 : out_0 + WINDOW * ROWS1],
                     lhsT=w_codes[u][:, o_cols].bitcast(FP8X4),
                     lhsT_scale=w_scales[u][:, o_cols],
                     rhs=x_codes[:, x_cols].bitcast(FP8X4),
@@ -157,10 +159,19 @@ def tile_butterflylayer2d_pb_s_kernel(tc, x_leaf, f_first, b_first, f_second, b_
                 n = node % WINDOW
                 nc.scalar.activation(
                     out=h_by_channel[:, node * ROWS2 : (node + 1) * ROWS2].rearrange("c m t -> c (m t)"),
-                    in_=h_ps[node // WINDOW][:, n, n * ROWS1 : (n + 1) * ROWS1],
+                    in_=h_ps[node // WINDOW][:, n * WINDOW * ROWS1 : n * WINDOW * ROWS1 + ROWS1],
                     func=RELU,
                     bias=b1_t[:, node : node + 1],
                 )
+
+        def add_bias_1(c):
+            first = c * WINDOW
+            nc.vector.tensor_tensor(
+                out=h_by_channel[:, first * ROWS2 : (first + WINDOW) * ROWS2].rearrange("c (n m) t -> c n (m t)", n=WINDOW),
+                in0=h_ps[c][:].rearrange("c (n r) -> c n r", n=WINDOW)[:, :, 0:ROWS1],
+                in1=b1_t[:, first : first + WINDOW].unsqueeze(2).to_broadcast([P, WINDOW, ROWS1]),
+                op=ADD,
+            )
 
         def keep_clock_up(passes):
             unread = psum.tile([P, NODES * ROWS1], F32, name="out_ps")
@@ -182,11 +193,12 @@ def tile_butterflylayer2d_pb_s_kernel(tc, x_leaf, f_first, b_first, f_second, b_
             keep_clock_up(2)
             turned = psum.tile([P, PACK, CH], BF16, name="turn_0")
             for place in range(PACK):
-                nc.tensor.transpose(turned[:, place, :], h_by_channel[:, :, place], ident_bf16[:])
+                q2, p2 = divmod(place, 2)
+                nc.tensor.transpose(turned[:, 2 * p2 + q2, :], h_by_channel[:, :, place], ident_bf16[:])
             return turned
 
         def keep_h_by_pixel(turned):
-            nc.vector.tensor_copy(out=h_by_pixel[:], in_=turned[:].rearrange("m t o -> m (t o)"))
+            nc.vector.tensor_scalar_max(h_by_pixel[:], turned[:].rearrange("m t o -> m (t o)"), 0.0)
 
         def turn_h_to_k_t():
             words = h_by_pixel[:].bitcast(F32).rearrange("m (k u) -> m k u", u=2)
@@ -229,64 +241,69 @@ def tile_butterflylayer2d_pb_s_kernel(tc, x_leaf, f_first, b_first, f_second, b_
                     stop=(stop and n == count - 1),
                 )
 
-        turn_x(0)
-        turn_x(1)
+        for x, bank in enumerate(("turn_0", "turn_1", "h_ps_0", "h_ps_1")):
+            turn_x(x, bank)
         copy(0)
         copy(1)
         quantise_x()
         bias_1()
         bias_2()
+        quantise(1)
+        keep_clock_up(3)
+        multiply_1(1)
         for u in range(2, 8, 2):
             copy(u)
             copy(u + 1)
-            quantise(u - 1)
-            if u == 2:
-                keep_clock_up(2)
-            multiply_1(u - 1)
+            if u > 2:
+                quantise(u - 1)
+                multiply_1(u - 1)
             quantise(u - 2)
-            keep_clock_up(1)
             multiply_1(u - 2)
+            keep_clock_up(1)
         copy(8)
         for u in range(4):
             finish_1(u)
         quantise(7)
         multiply_1(7)
         quantise(6)
-        keep_clock_up(1)
         multiply_1(6)
+        keep_clock_up(1)
+        add_bias_1(2)
         copy(9)
-        for u in range(4, 8):
-            finish_1(u)
-        copy(10)
-        copy(11)
+        add_bias_1(3)
+        quantise(8)
         turned = turn_h_to_pixels()
         keep_clock_up(2)
-        quantise(9)
-        quantise(8)
-        copy(12)
-        copy(13)
+        copy(10)
+        copy(11)
         keep_h_by_pixel(turned)
         turned_k = turn_h_to_k_t()
-        turn_h_to_k_s(turned_k)
+        quantise(9)
         quantise(11)
+        copy(12)
+        turn_h_to_k_s(turned_k)
         quantise(10)
-        copy(14)
-        copy(15)
+        copy(13)
         quantise_h()
         quantise(13)
         spread_h()
+        copy(14)
+        copy(15)
         quantise(12)
+        copy(16)
         out_ps = psum.tile([P, CH], F32)
-        multiply_2(9, out_ps, start=True)
-        for u in (8, 11, 10, 13, 12):
+        multiply_2(8, out_ps, start=True)
+        for u in (9, 11, 10, 13, 12):
             multiply_2(u, out_ps)
         quantise(15)
         multiply_2(15, out_ps)
         quantise(14)
-        multiply_2(14, out_ps, stop=True)
+        multiply_2(14, out_ps)
+        quantise(16)
+        multiply_2(16, out_ps, stop=True)
 
         biased = keep.tile([P, CH], F32)
         nc.vector.tensor_tensor(out=biased[:], in0=out_ps[:], in1=b2_rep[:], op=ADD)
         result = keep.tile([P, CH], F32)
-        nc.scalar.activation(out=result[:], in_=biased[:], func=RELU)
+        nc.vector.tensor_scalar_max(result[:], biased[:], 0.0)
         nc.sync.dma_start(out=out.rearrange("a b n y x o -> (a b n y x) o"), in_=result[:])

@@ -267,9 +267,8 @@ def tile_butterflylayer2d_pb_s_kernel(tc, x_leaf, f_first, b_first, f_second, b_
         multiply_1(7)
         quantise(6)
         multiply_1(6)
-        keep_clock_up(1)
-        add_bias_1(2)
         copy(9)
+        add_bias_1(2)
         add_bias_1(3)
         quantise(8)
         turned = turn_h_to_pixels()

@@ -190,7 +190,7 @@ def tile_butterflylayer2d_pb_s_kernel(tc, x_leaf, f_first, b_first, f_second, b_
         grouped_h = keep.tile([P, NODES * ROWS2 * PACK], BF16, align_bytes=64)
 
         def turn_h_to_pixels():
-            keep_clock_up(2)
+            keep_clock_up(1)
             turned = psum.tile([P, PACK, CH], BF16, name="turn_0")
             for place in range(PACK):
                 q2, p2 = divmod(place, 2)
@@ -259,7 +259,6 @@ def tile_butterflylayer2d_pb_s_kernel(tc, x_leaf, f_first, b_first, f_second, b_
                 multiply_1(u - 1)
             quantise(u - 2)
             multiply_1(u - 2)
-            keep_clock_up(1)
         copy(8)
         for u in range(4):
             finish_1(u)
@@ -272,7 +271,7 @@ def tile_butterflylayer2d_pb_s_kernel(tc, x_leaf, f_first, b_first, f_second, b_
         add_bias_1(3)
         quantise(8)
         turned = turn_h_to_pixels()
-        keep_clock_up(2)
+        keep_clock_up(1)
         copy(10)
         copy(11)
         keep_h_by_pixel(turned)

@@ -178,8 +178,8 @@ def tile_butterflylayer2d_pb_s_kernel(tc, x_leaf, f_first, b_first, f_second, b_
             for i in range(passes):
                 nc.tensor.matmul_mx(
                     out=unread[:],
-                    lhsT=w_codes[1][:, 0:CH].bitcast(FP8X4),
-                    lhsT_scale=w_scales[1][:, 0:CH],
+                    lhsT=w_codes[0][:, 0:CH].bitcast(FP8X4),
+                    lhsT_scale=w_scales[0][:, 0:CH],
                     rhs=x_codes[:].bitcast(FP8X4),
                     rhs_scale=x_scales[:],
                     start=True,
@@ -248,24 +248,34 @@ def tile_butterflylayer2d_pb_s_kernel(tc, x_leaf, f_first, b_first, f_second, b_
         quantise_x()
         bias_1()
         bias_2()
+        quantise(0)
+        multiply_1(0)
+        copy(2)
         quantise(1)
-        keep_clock_up(3)
         multiply_1(1)
-        for u in range(2, 8, 2):
-            copy(u)
-            copy(u + 1)
-            if u > 2:
-                quantise(u - 1)
-                multiply_1(u - 1)
-            quantise(u - 2)
-            multiply_1(u - 2)
+        keep_clock_up(3)
+        copy(3)
+        copy(4)
+        quantise(2)
+        multiply_1(2)
+        finish_1(0)
+        quantise(3)
+        multiply_1(3)
+        copy(5)
+        copy(6)
+        quantise(4)
+        multiply_1(4)
+        finish_1(1)
+        quantise(5)
+        multiply_1(5)
+        copy(7)
         copy(8)
-        for u in range(4):
-            finish_1(u)
-        quantise(7)
-        multiply_1(7)
         quantise(6)
         multiply_1(6)
+        quantise(7)
+        multiply_1(7)
+        finish_1(2)
+        finish_1(3)
         copy(9)
         add_bias_1(2)
         add_bias_1(3)

from contextlib import ExitStack

import concourse.mybir as mybir
from concourse.masks import make_identity

F32 = mybir.dt.float32
BF16 = mybir.dt.bfloat16
I32 = mybir.dt.int32
U32 = mybir.dt.uint32
U8 = mybir.dt.uint8
FP8X4 = mybir.dt.float8_e4m3fn_x4
RELU = mybir.ActivationFunctionType.Relu
ADD = mybir.AluOpType.add

P = 128
PACK = 4
NODES = 16
CH = 128
ROWS1 = 32
ROWS2 = 8
WINDOW = 4
DIAG = CH + ROWS2

FLOPS = 2 * NODES * (ROWS1 + ROWS2) * (PACK * CH) * CH

UNITS = [(level, node, 2, "sv"[node // 2 % 2]) for level in (1, 2) for node in range(0, NODES, 2)]
UNITS[-1:] = [(2, 14, 1, "v"), (2, 15, 1, "s")]


def regroup(copy, raw, grouped):
    copy(
        out=grouped[:].rearrange("p n (c i) t -> p n c t i", i=4),
        in_=raw[:].rearrange("p n t (c i) -> p n c t i", i=4),
    )


def tile_butterflylayer2d_pb_s_kernel(tc, x_leaf, f_first, b_first, f_second, b_second, out):
    nc = tc.nc
    with ExitStack() as ctx:
        keep = ctx.enter_context(tc.tile_pool(name="keep", bufs=1))
        psum = ctx.enter_context(tc.psum_pool(name="psum", bufs=1))
        ctx.enter_context(tc.manual_schedule())

        w_rows = {
            level: f.rearrange("a b p q (c t) o -> (p q c) (a b) t o", t=PACK)
            for level, f in ((1, f_first), (2, f_second))
        }
        raw = []
        for u, (level, node, count, engine) in enumerate(UNITS):
            raw.append(keep.tile([P, count, PACK, CH], BF16, name="raw_%d" % u))

        def load(u):
            level, node, count, engine = UNITS[u]
            nc.sync.dma_start(out=raw[u][:], in_=w_rows[level][:, node : node + count])

        x_sb = keep.tile([P, 4 * PACK * CH], BF16)
        x_rows = x_leaf.rearrange("a b n (y p) (x q) c -> x (a b n y) p (q c)", p=2, q=2)
        x_dst = x_sb[:].rearrange("r (x p w) -> r x p w", x=4, p=2)

        b_rows = keep.tile([P, CH], BF16)
        nc.vector.memset(b_rows[:], 0.0)
        for x in range(4):
            nc.sync.dma_start(out=x_dst[:, x], in_=x_rows[x])
        load(0)
        nc.sync.dma_start(out=b_rows[0:NODES, :], in_=b_first.rearrange("a b o -> (a b) o"))
        nc.sync.dma_start(out=b_rows[NODES : 2 * NODES, :], in_=b_second.rearrange("a b o -> (a b) o"))
        for u in range(1, len(UNITS)):
            load(u)

        ident_f32 = keep.tile([P, P], F32)
        make_identity(nc, ident_f32[:])
        ident_bf16 = keep.tile([P, P], BF16)
        make_identity(nc, ident_bf16[:])

        h_diag = keep.tile([P, NODES * DIAG], U32, align_bytes=64)
        nc.vector.memset(h_diag[:].bitcast(I32), 0)

        spread = keep.tile([P, NODES, ROWS2], BF16)
        nc.vector.tensor_copy(
            out=spread[:], in_=ident_bf16[:, NODES : 2 * NODES].unsqueeze(2).to_broadcast([P, NODES, ROWS2])
        )

        grouped = []
        w_codes = []
        w_scales = []
        for u, (level, node, count, engine) in enumerate(UNITS):
            grouped.append(keep.tile([P, count, CH, PACK], BF16, name="grouped_%d" % u, align_bytes=64))
            w_codes.append(keep.tile([P, count * CH], U32, name="w_codes_%d" % u, align_bytes=64))
            w_scales.append(keep.tile([P, count * CH], U8, name="w_scales_%d" % u, align_bytes=64))

        def copy(u):
            regroup(nc.scalar.copy if UNITS[u][3] == "s" else nc.vector.tensor_copy, raw[u], grouped[u])

        def quantise(u):
            nc.vector.quantize_mx(
                out=w_codes[u][:].bitcast(FP8X4),
                scales=w_scales[u][:],
                in_=grouped[u][:].rearrange("p n o t -> p (n o t)"),
            )

        x_words = x_sb[:].bitcast(F32).rearrange("r (x k u) -> r x k u", x=4, u=2)
        grouped_x = keep.tile([P, NODES * ROWS1 * PACK], BF16, align_bytes=64)
        gx_words = grouped_x[:].bitcast(F32).rearrange("k (m x q s u) -> k x q m s u", x=2, s=2, q=2, u=2)
        x_codes = keep.tile([P, NODES * ROWS1], U32, align_bytes=64)
        x_scales = keep.tile([P, NODES * ROWS1], U8, align_bytes=64)

        def turn_x(x, bank):
            xt = psum.tile([P, 2, P], F32, name=bank)
            for u in range(2):
                nc.tensor.transpose(xt[:, u, :], x_words[:, x, :, u], ident_f32[:])
            nc.vector.tensor_copy(
                out=gx_words[:, x // 2, x % 2], in_=xt[:].rearrange("k u (m s) -> k m s u", s=2)
            )

        def quantise_x():
            nc.vector.quantize_mx(out=x_codes[:].bitcast(FP8X4), scales=x_scales[:], in_=grouped_x[:])

        b1_t = keep.tile([P, NODES], F32)
        b2_rep = keep.tile([P, CH], F32)

        def bias_1():
            b1_ps = psum.tile([P, P], BF16, name="b_ps")
            nc.tensor.transpose(b1_ps[:], b_rows[:], ident_bf16[:])
            nc.scalar.copy(out=b1_t[:], in_=b1_ps[:, 0:NODES])

        def bias_2():
            b2_ps = psum.tile([P, CH], F32, name="h_ps_3")
            nc.tensor.matmul(
                b2_ps[:], lhsT=spread[:].rearrange("p n r -> p (n r)"), rhs=b_rows[:], start=True, stop=True
            )
            nc.scalar.copy(out=b2_rep[:], in_=b2_ps[:])

        h_by_channel = keep.tile([P, NODES * ROWS2, PACK], BF16)
        h_ps = {}

        def multiply_1(u):
            level, first, count, engine = UNITS[u]
            for n in range(count):
                node = first + n
                c = node // WINDOW
                if c not in h_ps:
                    h_ps[c] = psum.tile([P, WINDOW * WINDOW * ROWS1], F32, name="h_ps_%d" % c)
                out_0 = (node % WINDOW) * (WINDOW - 1) * ROWS1
                x_cols = slice(c * WINDOW * ROWS1, (c + 1) * WINDOW * ROWS1)
                o_cols = slice(n * CH, (n + 1) * CH)
                nc.tensor.matmul_mx(
                    out=h_ps[c][:, out_0 : out_0 + WINDOW * ROWS1],
                    lhsT=w_codes[u][:, o_cols].bitcast(FP8X4),
                    lhsT_scale=w_scales[u][:, o_cols],
                    rhs=x_codes[:, x_cols].bitcast(FP8X4),
                    rhs_scale=x_scales[:, x_cols],
                    start=True,
                    stop=True,
                )

        def finish_1(u):
            level, first, count, engine = UNITS[u]
            for node in range(first, first + count):
                n = node % WINDOW
                nc.scalar.activation(
                    out=h_by_channel[:, node * ROWS2 : (node + 1) * ROWS2].rearrange("c m t -> c (m t)"),
                    in_=h_ps[node // WINDOW][:, n * WINDOW * ROWS1 : n * WINDOW * ROWS1 + ROWS1],
                    func=RELU,
                    bias=b1_t[:, node : node + 1],
                )

        def add_bias_1(c):
            first = c * WINDOW
            nc.vector.tensor_tensor(
                out=h_by_channel[:, first * ROWS2 : (first + WINDOW) * ROWS2].rearrange("c (n m) t -> c n (m t)", n=WINDOW),
                in0=h_ps[c][:].rearrange("c (n r) -> c n r", n=WINDOW)[:, :, 0:ROWS1],
                in1=b1_t[:, first : first + WINDOW].unsqueeze(2).to_broadcast([P, WINDOW, ROWS1]),
                op=ADD,
            )

        def keep_clock_up(passes):
            unread = psum.tile([P, NODES * ROWS1], F32, name="out_ps")
            for i in range(passes):
                nc.tensor.matmul_mx(
                    out=unread[:],
                    lhsT=w_codes[0][:, 0:CH].bitcast(FP8X4),
                    lhsT_scale=w_scales[0][:, 0:CH],
                    rhs=x_codes[:].bitcast(FP8X4),
                    rhs_scale=x_scales[:],
                    start=True,
                    stop=True,
                )

        h_by_pixel = keep.tile([P, PACK * CH], BF16)
        grouped_h = keep.tile([P, NODES * ROWS2 * PACK], BF16, align_bytes=64)

        def turn_h_to_pixels():
            keep_clock_up(1)
            turned = psum.tile([P, PACK, CH], BF16, name="turn_0")
            for place in range(PACK):
                q2, p2 = divmod(place, 2)
                nc.tensor.transpose(turned[:, 2 * p2 + q2, :], h_by_channel[:, :, place], ident_bf16[:])
            return turned

        def keep_h_by_pixel(turned):
            nc.vector.tensor_scalar_max(h_by_pixel[:], turned[:].rearrange("m t o -> m (t o)"), 0.0)

        def turn_h_to_k_t():
            words = h_by_pixel[:].bitcast(F32).rearrange("m (k u) -> m k u", u=2)
            turned = psum.tile([P, 2, P], F32, name="turn_1")
            for u in range(2):
                nc.tensor.transpose(turned[:, u, :], words[:, :, u], ident_f32[:])
            keep_clock_up(3)
            return turned

        def turn_h_to_k_s(turned):
            nc.scalar.copy(
                out=grouped_h[:].bitcast(F32).rearrange("k (m u) -> k m u", u=2),
                in_=turned[:].rearrange("k u m -> k m u"),
            )

        h_codes = keep.tile([P, NODES * ROWS2], U32, align_bytes=64)
        h_scales = keep.tile([P, NODES * ROWS2], U8, align_bytes=64)

        def quantise_h():
            nc.vector.quantize_mx(out=h_codes[:].bitcast(FP8X4), scales=h_scales[:], in_=grouped_h[:])

        def spread_h():
            nc.vector.tensor_copy(
                out=h_diag[:].bitcast(I32).rearrange("k (i s) -> k i s", s=DIAG)[:, :, 0:ROWS2],
                in_=h_codes[:].bitcast(I32).rearrange("k (i s) -> k i s", s=ROWS2),
            )

        def multiply_2(u, out_ps, start=False, stop=False):
            level, first, count, engine = UNITS[u]
            for n in range(count):
                node = first + n
                o_cols = slice(n * CH, (n + 1) * CH)
                nc.tensor.matmul_mx(
                    out=out_ps[:],
                    lhsT=h_diag[:, node * CH : (node + 1) * CH].bitcast(FP8X4),
                    lhsT_scale=h_scales[:],
                    rhs=w_codes[u][:, o_cols].bitcast(FP8X4),
                    rhs_scale=w_scales[u][:, o_cols],
                    start=(start and n == 0),
                    stop=(stop and n == count - 1),
                )

        for x, bank in enumerate(("turn_0", "turn_1", "h_ps_0", "h_ps_1")):
            turn_x(x, bank)
        copy(0)
        copy(1)
        quantise_x()
        bias_1()
        bias_2()
        quantise(0)
        multiply_1(0)
        copy(2)
        quantise(1)
        multiply_1(1)
        keep_clock_up(3)
        copy(3)
        copy(4)
        quantise(2)
        multiply_1(2)
        finish_1(0)
        quantise(3)
        multiply_1(3)
        copy(5)
        copy(6)
        quantise(4)
        multiply_1(4)
        finish_1(1)
        quantise(5)
        multiply_1(5)
        copy(7)
        copy(8)
        quantise(6)
        multiply_1(6)
        quantise(7)
        multiply_1(7)
        finish_1(2)
        finish_1(3)
        copy(9)
        add_bias_1(2)
        add_bias_1(3)
        quantise(8)
        turned = turn_h_to_pixels()
        keep_clock_up(1)
        copy(10)
        copy(11)
        keep_h_by_pixel(turned)
        turned_k = turn_h_to_k_t()
        quantise(9)
        quantise(11)
        copy(12)
        turn_h_to_k_s(turned_k)
        quantise(10)
        copy(13)
        quantise_h()
        quantise(13)
        spread_h()
        copy(14)
        copy(15)
        quantise(12)
        copy(16)
        out_ps = psum.tile([P, CH], F32)
        multiply_2(8, out_ps, start=True)
        for u in (9, 11, 10, 13, 12):
            multiply_2(u, out_ps)
        quantise(15)
        multiply_2(15, out_ps)
        quantise(14)
        multiply_2(14, out_ps)
        quantise(16)
        multiply_2(16, out_ps, stop=True)

        biased = keep.tile([P, CH], F32)
        nc.vector.tensor_tensor(out=biased[:], in0=out_ps[:], in1=b2_rep[:], op=ADD)
        result = keep.tile([P, CH], F32)
        nc.vector.tensor_scalar_max(result[:], biased[:], 0.0)
        nc.sync.dma_start(out=out.rearrange("a b n y x o -> (a b n y x) o"), in_=result[:])
